import numpy as np
import ml_dtypes


def mxq(x, axis, fmt="e4m3"):
    dtype, down = {"e4m3": (ml_dtypes.float8_e4m3fn, 7), "e5m2": (ml_dtypes.float8_e5m2, 14)}[fmt]
    v = np.moveaxis(np.asarray(x, np.float32).astype(ml_dtypes.bfloat16).astype(np.float64), axis, -1)
    blocks = v.reshape(v.shape[:-1] + (-1, 32))
    amax = np.abs(blocks).max(-1, keepdims=True)
    byte = np.maximum(np.where(amax > 0, np.frexp(amax)[1] - 1 + 127, 0) - down, 1)
    scale = np.exp2(byte - 127.0)
    codes = (blocks / scale).astype(np.float32).astype(dtype).astype(np.float64)
    return np.moveaxis((codes * scale).reshape(v.shape), -1, axis)


WIDE = False


def mx_kscale(k):
    if not WIDE:
        return np.ones(k)
    levels = np.array([10, -10, 5, -5, 0])
    a = np.random.permutation(np.resize(levels, k // 512 * 4)).reshape(k // 512, 4)
    idx = np.arange(k)
    return np.exp2(a[idx // 512, idx % 128 // 32])


BF16 = ml_dtypes.bfloat16


def bf(x):
    return np.asarray(x, np.float32).astype(BF16)


def f64(x):
    return np.asarray(x).astype(np.float64)


B, T, E, V, H, C = 1, 1024, 1024, 2048, 8, 512
KD = E // H
ROPE_BASE = 10000.0


def rotate_every_two(u):
    u1 = u[..., ::2]
    u2 = u[..., 1::2]
    return np.stack((-u2, u1), axis=-1).reshape(u.shape)


def theta_shift(u, sin, cos):
    return u * cos + rotate_every_two(u) * sin


def setup_inputs():
    s = mx_kscale(E)
    angle = np.arange(T)[:, None] * (1.0 / ROPE_BASE ** (np.repeat(np.arange(KD // 2), 2) * 2.0 / KD))
    return {"x": bf(np.random.standard_normal((B, T, E)) * s),
            "sin": bf(np.sin(angle)), "cos": bf(np.cos(angle)),
            "Wq": bf(np.random.standard_normal((E, E)) * 0.5 / np.sqrt(E) / s[:, None]),
            "Wk": bf(np.random.standard_normal((E, E)) * 2.0 / np.sqrt(E) / s[:, None])}


def reference(x, sin, cos, Wq, Wk):
    xq = mxq(f64(x), 2, "e4m3")
    q = (xq @ mxq(f64(Wq), 0, "e4m3")).reshape(B, T, H, KD).transpose(0, 2, 1, 3)
    k = ((xq @ mxq(f64(Wk), 0, "e4m3")) * KD ** -0.5).reshape(B, T, H, KD).transpose(0, 2, 1, 3)
    return theta_shift(q, f64(sin), f64(cos)), theta_shift(k, f64(sin), f64(cos))

@@ -1,0 +1,189 @@
+from contextlib import ExitStack
+
+import concourse.mybir as mybir
+from concourse.masks import make_identity
+
+F32 = mybir.dt.float32
+BF16 = mybir.dt.bfloat16
+U32 = mybir.dt.uint32
+U8 = mybir.dt.uint8
+FP8X4 = mybir.dt.float8_e4m3fn_x4
+MULT = mybir.AluOpType.mult
+ADD = mybir.AluOpType.add
+
+P = 128
+POSITIONS = 1024
+K = 1024
+HEADS = 8
+CHANNELS = 128
+PAIRS = CHANNELS // 2
+PACK = 4
+K_PASS = P * PACK
+PASSES = K // K_PASS
+ROW_TILES = POSITIONS // P
+GROUP_HEADS = 4
+GROUP_COLS = GROUP_HEADS * CHANNELS
+PLANE = GROUP_COLS // 2
+GROUPS = 2 * HEADS // GROUP_HEADS
+STORE_TILES = 4
+K_SCALE = CHANNELS**-0.5
+
+FLOPS = 2 * 2 * POSITIONS * K * HEADS * CHANNELS
+
+
+def tile_multiscaleretention_pa_kernel(tc, x, sin, cos, Wq, Wk, out_0, out_1):
+    nc = tc.nc
+
+    x_rows = x.flatten_outer_dims().rearrange("(p j) k -> p j k", j=ROW_TILES)
+    cos_rows = cos.rearrange("(p j) d -> p j d", j=ROW_TILES)
+    sin_rows = sin.rearrange("(p j) d -> p j d", j=ROW_TILES)
+    out_rows = [o.rearrange("b h (p j) d -> p (b h) j d", j=ROW_TILES) for o in (out_0, out_1)]
+    w_rows = [w.rearrange("(c p t) n -> p c t n", c=PASSES, t=PACK) for w in (Wq, Wk)]
+
+    with ExitStack() as ctx:
+        keep = ctx.enter_context(tc.tile_pool(name="keep", bufs=1))
+        stage = ctx.enter_context(tc.tile_pool(name="stage", bufs=3))
+        psum_t = ctx.enter_context(tc.psum_pool(name="psum_t", bufs=2))
+        psum_acc = ctx.enter_context(tc.psum_pool(name="psum_acc", bufs=6))
+
+        x_sb = keep.tile([P, ROW_TILES, K], BF16)
+        tables_bf = keep.tile([P, 2, ROW_TILES, CHANNELS], BF16)
+        w_raw = [keep.tile([P, PASSES, PACK, GROUP_COLS], BF16, name="w_raw%d" % g) for g in range(GROUPS)]
+        x_codes = keep.tile([P, ROW_TILES, PASSES * P], U32, align_bytes=64)
+        x_scales = keep.tile([P, ROW_TILES, PASSES * P], U8, align_bytes=64)
+        w_codes = keep.tile([P, GROUPS, PASSES, GROUP_COLS], U32, align_bytes=64)
+        w_scales = keep.tile([P, GROUPS, PASSES, GROUP_COLS], U8, align_bytes=64)
+        factors = keep.tile([P, 2, ROW_TILES, 2, 2, PAIRS], F32)
+        identity = keep.tile([P, P], F32)
+
+        def load_x(first, last):
+            nc.sync.dma_start(out=x_sb[:, first:last, :], in_=x_rows[:, first:last, :])
+
+        def load_w(g):
+            cols = slice((g % 2) * GROUP_COLS, (g % 2 + 1) * GROUP_COLS)
+            for c in range(PASSES):
+                nc.sync.dma_start(out=w_raw[g][:, c, :, :], in_=w_rows[g // 2][:, c, :, cols])
+
+        nc.sync.dma_start(out=tables_bf[:, 0], in_=cos_rows)
+        nc.sync.dma_start(out=tables_bf[:, 1], in_=sin_rows)
+        load_x(0, 2)
+        load_w(0)
+        load_x(2, 4)
+        load_x(4, 8)
+        for g in range(1, GROUPS):
+            load_w(g)
+
+        make_identity(nc, identity[:])
+
+        def make_factors(engine, which, scale):
+            cos_pairs = tables_bf[:, 0].rearrange("p j (i e) -> p j i e", e=2)
+            sin_pairs = tables_bf[:, 1].rearrange("p j (i e) -> p j i e", e=2)
+            for source, e, table, sign in ((0, 0, cos_pairs, 1.0), (0, 1, sin_pairs, 1.0), (1, 0, sin_pairs, -1.0), (1, 1, cos_pairs, 1.0)):
+                engine.tensor_scalar(
+                    out=factors[:, which, :, source, e, :],
+                    in0=table[:, :, :, e],
+                    scalar1=sign * scale,
+                    scalar2=0.0,
+                    op0=MULT,
+                    op1=ADD,
+                )
+
+        make_factors(nc.vector, 0, 1.0)
+        make_factors(nc.gpsimd, 1, K_SCALE)
+
+        x_grouped = {}
+
+        def transpose_x(j):
+            words = x_sb[:, j, :].bitcast(F32)
+            turned = psum_t.tile([P, PASSES, 2, P], F32)
+            for c in range(PASSES):
+                for u in range(2):
+                    first = c * (K_PASS // 2) + u
+                    nc.tensor.transpose(turned[:, c, u, :], words[:, first : (c + 1) * (K_PASS // 2) : 2], identity[:])
+            grouped = stage.tile([P, PASSES * P * PACK], BF16, align_bytes=64, name="x_grouped")
+            nc.scalar.copy(
+                out=grouped[:].bitcast(F32).rearrange("p (c r u) -> p c r u", c=PASSES, u=2),
+                in_=turned[:].rearrange("p c u r -> p c r u"),
+            )
+            x_grouped[j] = grouped
+
+        def quantise_x(j):
+            nc.vector.quantize_mx(out=x_codes[:, j, :].bitcast(FP8X4), scales=x_scales[:, j, :], in_=x_grouped[j][:])
+
+        w_grouped = {}
+
+        def regroup_w(g, c, engines):
+            grouped = stage.tile([P, 2, PLANE, PACK], BF16, align_bytes=64, name="w_grouped", bufs=2)
+            source = w_raw[g][:, c].rearrange("p t (m e) -> p e m t", e=2)
+            for e in range(2):
+                if engines[e] == "vector":
+                    nc.vector.tensor_copy(out=grouped[:, e], in_=source[:, e])
+                else:
+                    nc.scalar.copy(out=grouped[:, e], in_=source[:, e])
+            w_grouped[(g, c)] = grouped
+
+        def quantise_w(g, c):
+            nc.vector.quantize_mx(
+                out=w_codes[:, g, c, :].bitcast(FP8X4),
+                scales=w_scales[:, g, c, :],
+                in_=w_grouped[(g, c)][:].rearrange("p e m t -> p (e m t)"),
+            )
+
+        rotated = {}
+
+        def project_and_rotate(g, j):
+            acc = psum_acc.tile([P, GROUP_COLS], F32)
+            for c in range(PASSES):
+                rows = slice(c * P, (c + 1) * P)
+                nc.tensor.matmul_mx(
+                    out=acc[:],
+                    lhsT=x_codes[:, j, rows].bitcast(FP8X4),
+                    lhsT_scale=x_scales[:, j, rows],
+                    rhs=w_codes[:, g, c, :].bitcast(FP8X4),
+                    rhs_scale=w_scales[:, g, c, :],
+                    start=(c == 0),
+                    stop=(c == PASSES - 1),
+                )
+            shape = [P, 2, GROUP_HEADS, PAIRS]
+            parts = []
+            for source in range(2):
+                part = stage.tile(shape, F32, name="part%d" % source)
+                plane = acc[:, source * PLANE : (source + 1) * PLANE].rearrange("p (h i) -> p h i", h=GROUP_HEADS)
+                nc.vector.tensor_tensor(
+                    out=part[:],
+                    in0=plane.unsqueeze(1).to_broadcast(shape),
+                    in1=factors[:, g // 2, j, source].unsqueeze(2).to_broadcast(shape),
+                    op=MULT,
+                )
+                parts.append(part)
+            slot = j % STORE_TILES
+            if slot == 0:
+                rotated[g] = stage.tile([P, GROUP_HEADS, STORE_TILES, CHANNELS], F32, name="rotated")
+            nc.gpsimd.tensor_tensor(
+                out=rotated[g][:, :, slot, :].rearrange("p h (i e) -> p h i e", e=2),
+                in0=parts[0][:].rearrange("p e h i -> p h i e"),
+                in1=parts[1][:].rearrange("p e h i -> p h i e"),
+                op=ADD,
+            )
+            if slot == STORE_TILES - 1:
+                heads = slice((g % 2) * GROUP_HEADS, (g % 2 + 1) * GROUP_HEADS)
+                nc.sync.dma_start(out=out_rows[g // 2][:, heads, j - slot : j + 1, :], in_=rotated[g][:])
+
+        transpose_x(0)
+        transpose_x(1)
+        regroup_w(0, 0, ("vector", "vector"))
+        regroup_w(0, 1, ("vector", "scalar"))
+        quantise_x(0)
+        quantise_w(0, 0)
+        quantise_w(0, 1)
+        for g in range(GROUPS):
+            for j in range(ROW_TILES):
+                if g == 0 and j + 2 < ROW_TILES:
+                    transpose_x(j + 2)
+                if g == 0 and j + 1 < ROW_TILES:
+                    quantise_x(j + 1)
+                if g + 1 < GROUPS and j < PASSES:
+                    regroup_w(g + 1, j, ("scalar", "scalar"))
+                if g + 1 < GROUPS and j >= ROW_TILES - PASSES:
+                    quantise_w(g + 1, j - (ROW_TILES - PASSES))
+                project_and_rotate(g, j)

@@ -23,7 +23,7 @@ PASSES = K // K_PASS
 ROW_TILES = POSITIONS // P
 GROUP_HEADS = 4
 GROUP_COLS = GROUP_HEADS * CHANNELS
-PLANE = GROUP_COLS // 2
+RUN = 4
 GROUPS = 2 * HEADS // GROUP_HEADS
 STORE_TILES = 4
 K_SCALE = CHANNELS**-0.5
@@ -112,21 +112,22 @@ def tile_multiscaleretention_pa_kernel(tc, x, sin, cos, Wq, Wk, out_0, out_1):
 
         w_grouped = {}
 
-        def regroup_w(g, c, engines):
-            grouped = stage.tile([P, 2, PLANE, PACK], BF16, align_bytes=64, name="w_grouped", bufs=2)
-            source = w_raw[g][:, c].rearrange("p t (m e) -> p e m t", e=2)
-            for e in range(2):
-                if engines[e] == "vector":
-                    nc.vector.tensor_copy(out=grouped[:, e], in_=source[:, e])
-                else:
-                    nc.scalar.copy(out=grouped[:, e], in_=source[:, e])
+        def regroup_w(g, c, copies):
+            grouped = stage.tile([P, GROUP_COLS, PACK], BF16, align_bytes=64, name="w_grouped", bufs=2)
+            half = GROUP_COLS // 2
+            for part, copy in enumerate(copies):
+                cols = slice(part * half, (part + 1) * half)
+                copy(
+                    out=grouped[:, cols, :].rearrange("p (n r) t -> p n t r", r=RUN),
+                    in_=w_raw[g][:, c, :, cols].rearrange("p t (n r) -> p n t r", r=RUN),
+                )
             w_grouped[(g, c)] = grouped
 
         def quantise_w(g, c):
             nc.vector.quantize_mx(
                 out=w_codes[:, g, c, :].bitcast(FP8X4),
                 scales=w_scales[:, g, c, :],
-                in_=w_grouped[(g, c)][:].rearrange("p e m t -> p (e m t)"),
+                in_=w_grouped[(g, c)][:].rearrange("p n t -> p (n t)"),
             )
 
         rotated = {}
@@ -144,35 +145,30 @@ def tile_multiscaleretention_pa_kernel(tc, x, sin, cos, Wq, Wk, out_0, out_1):
                     start=(c == 0),
                     stop=(c == PASSES - 1),
                 )
-            shape = [P, 2, GROUP_HEADS, PAIRS]
-            parts = []
-            for source in range(2):
-                part = stage.tile(shape, F32, name="part%d" % source)
-                plane = acc[:, source * PLANE : (source + 1) * PLANE].rearrange("p (h i) -> p h i", h=GROUP_HEADS)
-                nc.vector.tensor_tensor(
-                    out=part[:],
-                    in0=plane.unsqueeze(1).to_broadcast(shape),
-                    in1=factors[:, g // 2, j, source].unsqueeze(2).to_broadcast(shape),
-                    op=MULT,
-                )
-                parts.append(part)
             slot = j % STORE_TILES
             if slot == 0:
-                rotated[g] = stage.tile([P, GROUP_HEADS, STORE_TILES, CHANNELS], F32, name="rotated")
-            nc.gpsimd.tensor_tensor(
-                out=rotated[g][:, :, slot, :].rearrange("p h (i e) -> p h i e", e=2),
-                in0=parts[0][:].rearrange("p e h i -> p h i e"),
-                in1=parts[1][:].rearrange("p e h i -> p h i e"),
-                op=ADD,
-            )
+                rotated[g] = [
+                    stage.tile([P, GROUP_HEADS, STORE_TILES, CHANNELS], F32, name="share%d" % source) for source in range(2)
+                ]
+            shape = [P, GROUP_HEADS, PAIRS, 2]
+            pairs = acc[:].rearrange("p (h i e) -> p h i e", h=GROUP_HEADS, e=2)
+            shares = [tile[:, :, slot, :] for tile in rotated[g]]
+            for source in range(2):
+                nc.vector.tensor_tensor(
+                    out=shares[source].rearrange("p h (i e) -> p h i e", e=2),
+                    in0=pairs[:, :, :, source : source + 1].to_broadcast(shape),
+                    in1=factors[:, g // 2, j, source].rearrange("p e i -> p i e").unsqueeze(1).to_broadcast(shape),
+                    op=MULT,
+                )
+            nc.gpsimd.tensor_tensor(out=shares[0], in0=shares[0], in1=shares[1], op=ADD)
             if slot == STORE_TILES - 1:
                 heads = slice((g % 2) * GROUP_HEADS, (g % 2 + 1) * GROUP_HEADS)
-                nc.sync.dma_start(out=out_rows[g // 2][:, heads, j - slot : j + 1, :], in_=rotated[g][:])
+                nc.sync.dma_start(out=out_rows[g // 2][:, heads, j - slot : j + 1, :], in_=rotated[g][0][:])
 
         transpose_x(0)
         transpose_x(1)
-        regroup_w(0, 0, ("vector", "vector"))
-        regroup_w(0, 1, ("vector", "scalar"))
+        regroup_w(0, 0, (nc.vector.tensor_copy, nc.vector.tensor_copy))
+        regroup_w(0, 1, (nc.vector.tensor_copy, nc.scalar.copy))
         quantise_x(0)
         quantise_w(0, 0)
         quantise_w(0, 1)
@@ -183,7 +179,7 @@ def tile_multiscaleretention_pa_kernel(tc, x, sin, cos, Wq, Wk, out_0, out_1):
                 if g == 0 and j + 1 < ROW_TILES:
                     quantise_x(j + 1)
                 if g + 1 < GROUPS and j < PASSES:
-                    regroup_w(g + 1, j, ("scalar", "scalar"))
+                    regroup_w(g + 1, j, (nc.scalar.copy, nc.scalar.copy))
                 if g + 1 < GROUPS and j >= ROW_TILES - PASSES:
                     quantise_w(g + 1, j - (ROW_TILES - PASSES))
                 project_and_rotate(g, j)

@@ -160,8 +160,8 @@ def tile_multiscaleretention_pa_kernel(tc, x, sin, cos, Wq, Wk, out_0, out_1):
                     in1=factors[:, g // 2, j, source].rearrange("p e i -> p i e").unsqueeze(1).to_broadcast(shape),
                     op=MULT,
                 )
-            nc.gpsimd.tensor_tensor(out=shares[0], in0=shares[0], in1=shares[1], op=ADD)
             if slot == STORE_TILES - 1:
+                nc.gpsimd.tensor_tensor(out=rotated[g][0][:], in0=rotated[g][0][:], in1=rotated[g][1][:], op=ADD)
                 heads = slice((g % 2) * GROUP_HEADS, (g % 2 + 1) * GROUP_HEADS)
                 nc.sync.dma_start(out=out_rows[g // 2][:, heads, j - slot : j + 1, :], in_=rotated[g][0][:])
 

@@ -160,8 +160,9 @@ def tile_multiscaleretention_pa_kernel(tc, x, sin, cos, Wq, Wk, out_0, out_1):
                     in1=factors[:, g // 2, j, source].rearrange("p e i -> p i e").unsqueeze(1).to_broadcast(shape),
                     op=MULT,
                 )
+            adder = nc.vector if slot == STORE_TILES - 1 else nc.gpsimd
+            adder.tensor_tensor(out=shares[0], in0=shares[0], in1=shares[1], op=ADD)
             if slot == STORE_TILES - 1:
-                nc.gpsimd.tensor_tensor(out=rotated[g][0][:], in0=rotated[g][0][:], in1=rotated[g][1][:], op=ADD)
                 heads = slice((g % 2) * GROUP_HEADS, (g % 2 + 1) * GROUP_HEADS)
                 nc.sync.dma_start(out=out_rows[g // 2][:, heads, j - slot : j + 1, :], in_=rotated[g][0][:])
 

@@ -10,6 +10,7 @@ U8 = mybir.dt.uint8
 FP8X4 = mybir.dt.float8_e4m3fn_x4
 MULT = mybir.AluOpType.mult
 ADD = mybir.AluOpType.add
+COPY = mybir.ActivationFunctionType.Copy
 
 P = 128
 POSITIONS = 1024
@@ -25,7 +26,9 @@ GROUP_HEADS = 4
 GROUP_COLS = GROUP_HEADS * CHANNELS
 RUN = 4
 GROUPS = 2 * HEADS // GROUP_HEADS
-STORE_TILES = 4
+TILES = GROUPS * ROW_TILES
+UNIT_TILES = 2
+TABLE_PARTS = ((0, 2), (2, ROW_TILES))
 K_SCALE = CHANNELS**-0.5
 
 FLOPS = 2 * 2 * POSITIONS * K * HEADS * CHANNELS
@@ -35,8 +38,8 @@ def tile_multiscaleretention_pa_kernel(tc, x, sin, cos, Wq, Wk, out_0, out_1):
     nc = tc.nc
 
     x_rows = x.flatten_outer_dims().rearrange("(p j) k -> p j k", j=ROW_TILES)
-    cos_rows = cos.rearrange("(p j) d -> p j d", j=ROW_TILES)
-    sin_rows = sin.rearrange("(p j) d -> p j d", j=ROW_TILES)
+    cos_rows = cos.rearrange("(p j) d -> p (j d)", j=ROW_TILES)
+    sin_rows = sin.rearrange("(p j) d -> p (j d)", j=ROW_TILES)
     out_rows = [o.rearrange("b h (p j) d -> p (b h) j d", j=ROW_TILES) for o in (out_0, out_1)]
     w_rows = [w.rearrange("(c p t) n -> p c t n", c=PASSES, t=PACK) for w in (Wq, Wk)]
 
@@ -45,51 +48,74 @@ def tile_multiscaleretention_pa_kernel(tc, x, sin, cos, Wq, Wk, out_0, out_1):
         stage = ctx.enter_context(tc.tile_pool(name="stage", bufs=3))
         psum_t = ctx.enter_context(tc.psum_pool(name="psum_t", bufs=2))
         psum_acc = ctx.enter_context(tc.psum_pool(name="psum_acc", bufs=6))
+        ctx.enter_context(tc.manual_schedule())
 
         x_sb = keep.tile([P, ROW_TILES, K], BF16)
-        tables_bf = keep.tile([P, 2, ROW_TILES, CHANNELS], BF16)
+        tables = [keep.tile([P, 3 * (last - first) * CHANNELS + 2], BF16, name="tables%d" % first) for first, last in TABLE_PARTS]
         w_raw = [keep.tile([P, PASSES, PACK, GROUP_COLS], BF16, name="w_raw%d" % g) for g in range(GROUPS)]
         x_codes = keep.tile([P, ROW_TILES, PASSES * P], U32, align_bytes=64)
         x_scales = keep.tile([P, ROW_TILES, PASSES * P], U8, align_bytes=64)
         w_codes = keep.tile([P, GROUPS, PASSES, GROUP_COLS], U32, align_bytes=64)
         w_scales = keep.tile([P, GROUPS, PASSES, GROUP_COLS], U8, align_bytes=64)
-        factors = keep.tile([P, 2, ROW_TILES, 2, 2, PAIRS], F32)
+        factors = keep.tile([P, 2, ROW_TILES, 2, CHANNELS], F32)
         identity = keep.tile([P, P], F32)
 
         def load_x(first, last):
             nc.sync.dma_start(out=x_sb[:, first:last, :], in_=x_rows[:, first:last, :])
 
-        def load_w(g):
+        def load_w(g, c):
             cols = slice((g % 2) * GROUP_COLS, (g % 2 + 1) * GROUP_COLS)
-            for c in range(PASSES):
-                nc.sync.dma_start(out=w_raw[g][:, c, :, :], in_=w_rows[g // 2][:, c, :, cols])
+            nc.sync.dma_start(out=w_raw[g][:, c, :, :], in_=w_rows[g // 2][:, c, :, cols])
 
-        nc.sync.dma_start(out=tables_bf[:, 0], in_=cos_rows)
-        nc.sync.dma_start(out=tables_bf[:, 1], in_=sin_rows)
-        load_x(0, 2)
-        load_w(0)
+        def load_tables(part):
+            first, last = TABLE_PARTS[part]
+            length = (last - first) * CHANNELS
+            for place, rows in enumerate((cos_rows, sin_rows, cos_rows)):
+                nc.sync.dma_start(
+                    out=tables[part][:, place * length : (place + 1) * length],
+                    in_=rows[:, first * CHANNELS : last * CHANNELS],
+                )
+
+        load_x(0, 1)
+        load_w(0, 0)
+        load_w(0, 1)
+        load_tables(0)
+        load_x(1, 2)
         load_x(2, 4)
-        load_x(4, 8)
-        for g in range(1, GROUPS):
-            load_w(g)
+        load_tables(1)
+        load_x(4, 6)
+        load_w(1, 0)
+        load_x(6, 8)
+        load_w(1, 1)
+        for g in range(2, GROUPS):
+            for c in range(PASSES):
+                load_w(g, c)
 
         make_identity(nc, identity[:])
 
-        def make_factors(engine, which, scale):
-            cos_pairs = tables_bf[:, 0].rearrange("p j (i e) -> p j i e", e=2)
-            sin_pairs = tables_bf[:, 1].rearrange("p j (i e) -> p j i e", e=2)
-            for source, e, table, sign in ((0, 0, cos_pairs, 1.0), (0, 1, sin_pairs, 1.0), (1, 0, sin_pairs, -1.0), (1, 1, cos_pairs, 1.0)):
-                engine.tensor_scalar(
-                    out=factors[:, which, :, source, e, :],
-                    in0=table[:, :, :, e],
-                    scalar1=sign * scale,
+        def make_q_factors(part):
+            first, last = TABLE_PARTS[part]
+            length = (last - first) * CHANNELS
+            sin_even = tables[part][:, length : 2 * length].rearrange("p (w z) -> p w z", z=2)[:, :, 0]
+            nc.gpsimd.tensor_scalar(out=sin_even, in0=sin_even, scalar1=-1.0, scalar2=0.0, op0=MULT, op1=ADD)
+            for source in range(2):
+                both = tables[part][:, source * length : source * length + 2 * (length + 1)].rearrange("p (e w) -> p e w", e=2)
+                nc.gpsimd.tensor_scalar(
+                    out=factors[:, 0, first:last, source, :].rearrange("p j (i e) -> p j i e", e=2),
+                    in0=both[:, :, 0:length].rearrange("p e (j i z) -> p j i z e", i=PAIRS, z=2)[:, :, :, 0, :],
+                    scalar1=1.0,
                     scalar2=0.0,
                     op0=MULT,
                     op1=ADD,
                 )
 
-        make_factors(nc.vector, 0, 1.0)
-        make_factors(nc.gpsimd, 1, K_SCALE)
+        def make_k_factors():
+            nc.scalar.activation(
+                out=factors[:, 1].rearrange("p j s d -> p (j s d)"),
+                in_=factors[:, 0].rearrange("p j s d -> p (j s d)"),
+                func=COPY,
+                scale=K_SCALE,
+            )
 
         x_grouped = {}
 
@@ -100,7 +126,7 @@ def tile_multiscaleretention_pa_kernel(tc, x, sin, cos, Wq, Wk, out_0, out_1):
                 for u in range(2):
                     first = c * (K_PASS // 2) + u
                     nc.tensor.transpose(turned[:, c, u, :], words[:, first : (c + 1) * (K_PASS // 2) : 2], identity[:])
-            grouped = stage.tile([P, PASSES * P * PACK], BF16, align_bytes=64, name="x_grouped")
+            grouped = stage.tile([P, PASSES * P * PACK], BF16, align_bytes=64, name="x_grouped", bufs=4)
             nc.scalar.copy(
                 out=grouped[:].bitcast(F32).rearrange("p (c r u) -> p c r u", c=PASSES, u=2),
                 in_=turned[:].rearrange("p c u r -> p c r u"),
@@ -112,27 +138,27 @@ def tile_multiscaleretention_pa_kernel(tc, x, sin, cos, Wq, Wk, out_0, out_1):
 
         w_grouped = {}
 
-        def regroup_w(g, c, copies):
-            grouped = stage.tile([P, GROUP_COLS, PACK], BF16, align_bytes=64, name="w_grouped", bufs=2)
+        def regroup_w(g, c, part, copy):
+            if (c, part) == (0, 0):
+                w_grouped[g] = stage.tile([P, PASSES, GROUP_COLS, PACK], BF16, align_bytes=64, name="w_grouped", bufs=2)
             half = GROUP_COLS // 2
-            for part, copy in enumerate(copies):
-                cols = slice(part * half, (part + 1) * half)
-                copy(
-                    out=grouped[:, cols, :].rearrange("p (n r) t -> p n t r", r=RUN),
-                    in_=w_raw[g][:, c, :, cols].rearrange("p t (n r) -> p n t r", r=RUN),
-                )
-            w_grouped[(g, c)] = grouped
+            cols = slice(part * half, (part + 1) * half)
+            copy(
+                out=w_grouped[g][:, c, cols, :].rearrange("p (n r) t -> p n t r", r=RUN),
+                in_=w_raw[g][:, c, :, cols].rearrange("p t (n r) -> p n t r", r=RUN),
+            )
 
-        def quantise_w(g, c):
+        def quantise_w_pass(g, c):
             nc.vector.quantize_mx(
                 out=w_codes[:, g, c, :].bitcast(FP8X4),
                 scales=w_scales[:, g, c, :],
-                in_=w_grouped[(g, c)][:].rearrange("p n t -> p (n t)"),
+                in_=w_grouped[g][:, c].rearrange("p n t -> p (n t)"),
             )
 
-        rotated = {}
+        sums = {}
 
-        def project_and_rotate(g, j):
+        def project(n):
+            g, j = divmod(n, ROW_TILES)
             acc = psum_acc.tile([P, GROUP_COLS], F32)
             for c in range(PASSES):
                 rows = slice(c * P, (c + 1) * P)
@@ -145,42 +171,68 @@ def tile_multiscaleretention_pa_kernel(tc, x, sin, cos, Wq, Wk, out_0, out_1):
                     start=(c == 0),
                     stop=(c == PASSES - 1),
                 )
-            slot = j % STORE_TILES
-            if slot == 0:
-                rotated[g] = [
-                    stage.tile([P, GROUP_HEADS, STORE_TILES, CHANNELS], F32, name="share%d" % source) for source in range(2)
-                ]
-            shape = [P, GROUP_HEADS, PAIRS, 2]
-            pairs = acc[:].rearrange("p (h i e) -> p h i e", h=GROUP_HEADS, e=2)
-            shares = [tile[:, :, slot, :] for tile in rotated[g]]
-            for source in range(2):
-                nc.vector.tensor_tensor(
-                    out=shares[source].rearrange("p h (i e) -> p h i e", e=2),
-                    in0=pairs[:, :, :, source : source + 1].to_broadcast(shape),
-                    in1=factors[:, g // 2, j, source].rearrange("p e i -> p i e").unsqueeze(1).to_broadcast(shape),
-                    op=MULT,
-                )
-            adder = nc.vector if slot == STORE_TILES - 1 else nc.gpsimd
-            adder.tensor_tensor(out=shares[0], in0=shares[0], in1=shares[1], op=ADD)
-            if slot == STORE_TILES - 1:
-                heads = slice((g % 2) * GROUP_HEADS, (g % 2 + 1) * GROUP_HEADS)
-                nc.sync.dma_start(out=out_rows[g // 2][:, heads, j - slot : j + 1, :], in_=rotated[g][0][:])
+            sums[n] = acc
+
+        def store_unit(n):
+            j = n % ROW_TILES
+            if n >= TILES - UNIT_TILES:
+                return j, j + 1
+            first = j - j % UNIT_TILES
+            return first, first + UNIT_TILES
+
+        shares = {}
+
+        def rotate(n):
+            g, j = divmod(n, ROW_TILES)
+            first, last = store_unit(n)
+            if j == first:
+                shares[g] = stage.tile([P, 2, GROUP_HEADS, last - first, CHANNELS], F32, name="shares", bufs=6)
+            shape = [P, 2, GROUP_HEADS, PAIRS, 2]
+            nc.vector.tensor_tensor(
+                out=shares[g][:, :, :, j - first, :].rearrange("p s h (i e) -> p s h i e", e=2),
+                in0=sums[n][:].rearrange("p (h i s) -> p s h i", h=GROUP_HEADS, s=2).unsqueeze(4).to_broadcast(shape),
+                in1=factors[:, g // 2, j].rearrange("p s (i e) -> p s i e", e=2).unsqueeze(2).to_broadcast(shape),
+                op=MULT,
+            )
+
+        def add_and_store(engine, n):
+            g = n // ROW_TILES
+            first, last = store_unit(n)
+            engine.tensor_tensor(out=shares[g][:, 0], in0=shares[g][:, 0], in1=shares[g][:, 1], op=ADD)
+            heads = slice((g % 2) * GROUP_HEADS, (g % 2 + 1) * GROUP_HEADS)
+            nc.sync.dma_start(out=out_rows[g // 2][:, heads, first:last, :], in_=shares[g][:, 0])
 
         transpose_x(0)
-        transpose_x(1)
-        regroup_w(0, 0, (nc.vector.tensor_copy, nc.vector.tensor_copy))
-        regroup_w(0, 1, (nc.vector.tensor_copy, nc.scalar.copy))
+        regroup_w(0, 0, 0, nc.vector.tensor_copy)
+        regroup_w(0, 0, 1, nc.scalar.copy)
         quantise_x(0)
-        quantise_w(0, 0)
-        quantise_w(0, 1)
-        for g in range(GROUPS):
-            for j in range(ROW_TILES):
-                if g == 0 and j + 2 < ROW_TILES:
-                    transpose_x(j + 2)
-                if g == 0 and j + 1 < ROW_TILES:
-                    quantise_x(j + 1)
-                if g + 1 < GROUPS and j < PASSES:
-                    regroup_w(g + 1, j, (nc.scalar.copy, nc.scalar.copy))
-                if g + 1 < GROUPS and j >= ROW_TILES - PASSES:
-                    quantise_w(g + 1, j - (ROW_TILES - PASSES))
-                project_and_rotate(g, j)
+        regroup_w(0, 1, 0, nc.vector.tensor_copy)
+        regroup_w(0, 1, 1, nc.scalar.copy)
+        transpose_x(1)
+        quantise_w_pass(0, 0)
+        quantise_w_pass(0, 1)
+        quantise_x(1)
+        make_q_factors(0)
+        project(0)
+        transpose_x(2)
+        transpose_x(3)
+        project(1)
+        make_q_factors(1)
+        for n in range(TILES):
+            g, j = divmod(n, ROW_TILES)
+            if n % 2 == 0 and n + 4 < ROW_TILES:
+                transpose_x(n + 4)
+                transpose_x(n + 5)
+            if g + 1 < GROUPS and 1 <= j <= 2 * PASSES:
+                regroup_w(g + 1, (j - 1) // 2, (j - 1) % 2, nc.scalar.copy)
+            if n == ROW_TILES + 2 * PASSES + 1:
+                make_k_factors()
+            rotate(n)
+            if n + 2 < ROW_TILES:
+                quantise_x(n + 2)
+            if g + 1 < GROUPS and j >= ROW_TILES - 1 - PASSES and j < ROW_TILES - 1:
+                quantise_w_pass(g + 1, j - (ROW_TILES - 1 - PASSES))
+            if n + 2 < TILES:
+                project(n + 2)
+            if j + 1 == store_unit(n)[1]:
+                add_and_store(nc.vector if n >= TILES - UNIT_TILES else nc.gpsimd, n)

@@ -28,6 +28,9 @@ RUN = 4
 GROUPS = 2 * HEADS // GROUP_HEADS
 TILES = GROUPS * ROW_TILES
 UNIT_TILES = 2
+UNITS = ((0, 2), (2, 3), (3, 5), (5, 6), (6, 8))
+AHEAD = 3
+VECTOR_ADDS = 4
 TABLE_PARTS = ((0, 2), (2, ROW_TILES))
 K_SCALE = CHANNELS**-0.5
 
@@ -121,7 +124,7 @@ def tile_multiscaleretention_pa_kernel(tc, x, sin, cos, Wq, Wk, out_0, out_1):
 
         def transpose_x(j):
             words = x_sb[:, j, :].bitcast(F32)
-            turned = psum_t.tile([P, PASSES, 2, P], F32)
+            turned = psum_t.tile([P, PASSES, 2, P], F32, name="turned")
             for c in range(PASSES):
                 for u in range(2):
                     first = c * (K_PASS // 2) + u
@@ -146,6 +149,13 @@ def tile_multiscaleretention_pa_kernel(tc, x, sin, cos, Wq, Wk, out_0, out_1):
             copy(
                 out=w_grouped[g][:, c, cols, :].rearrange("p (n r) t -> p n t r", r=RUN),
                 in_=w_raw[g][:, c, :, cols].rearrange("p t (n r) -> p n t r", r=RUN),
+            )
+
+        def quantise_w(g):
+            nc.vector.quantize_mx(
+                out=w_codes[:, g].rearrange("p c n -> p (c n)").bitcast(FP8X4),
+                scales=w_scales[:, g].rearrange("p c n -> p (c n)"),
+                in_=w_grouped[g][:].rearrange("p c n t -> p (c n t)"),
             )
 
         def quantise_w_pass(g, c):
@@ -177,6 +187,8 @@ def tile_multiscaleretention_pa_kernel(tc, x, sin, cos, Wq, Wk, out_0, out_1):
             j = n % ROW_TILES
             if n >= TILES - UNIT_TILES:
                 return j, j + 1
+            if n >= ROW_TILES:
+                return [unit for unit in UNITS if unit[0] <= j < unit[1]][0]
             first = j - j % UNIT_TILES
             return first, first + UNIT_TILES
 
@@ -186,21 +198,43 @@ def tile_multiscaleretention_pa_kernel(tc, x, sin, cos, Wq, Wk, out_0, out_1):
             g, j = divmod(n, ROW_TILES)
             first, last = store_unit(n)
             if j == first:
-                shares[g] = stage.tile([P, 2, GROUP_HEADS, last - first, CHANNELS], F32, name="shares", bufs=6)
+                shares[n - j + first] = stage.tile([P, 2, GROUP_HEADS, last - first, CHANNELS], F32, name="shares", bufs=6)
             shape = [P, 2, GROUP_HEADS, PAIRS, 2]
             nc.vector.tensor_tensor(
-                out=shares[g][:, :, :, j - first, :].rearrange("p s h (i e) -> p s h i e", e=2),
+                out=shares[n - j + first][:, :, :, j - first, :].rearrange("p s h (i e) -> p s h i e", e=2),
                 in0=sums[n][:].rearrange("p (h i s) -> p s h i", h=GROUP_HEADS, s=2).unsqueeze(4).to_broadcast(shape),
                 in1=factors[:, g // 2, j].rearrange("p s (i e) -> p s i e", e=2).unsqueeze(2).to_broadcast(shape),
                 op=MULT,
             )
 
         def add_and_store(engine, n):
-            g = n // ROW_TILES
+            j = n % ROW_TILES
+            unit = shares[n - j + store_unit(n)[0]]
+            engine.tensor_tensor(out=unit[:, 0], in0=unit[:, 0], in1=unit[:, 1], op=ADD)
+            store(n)
+
+        def store(n):
+            g, j = divmod(n, ROW_TILES)
             first, last = store_unit(n)
-            engine.tensor_tensor(out=shares[g][:, 0], in0=shares[g][:, 0], in1=shares[g][:, 1], op=ADD)
             heads = slice((g % 2) * GROUP_HEADS, (g % 2 + 1) * GROUP_HEADS)
-            nc.sync.dma_start(out=out_rows[g // 2][:, heads, first:last, :], in_=shares[g][:, 0])
+            nc.sync.dma_start(out=out_rows[g // 2][:, heads, first:last, :], in_=shares[n - j + first][:, 0])
+
+        summed = {}
+
+        def add_on_tensor(n):
+            summed[n] = psum_t.tile([P, GROUP_COLS], F32, name="turned")
+            for source in range(2):
+                nc.tensor.matmul(
+                    out=summed[n][:],
+                    lhsT=identity[:],
+                    rhs=shares[n][:, source].rearrange("p h u d -> p (h u d)"),
+                    start=(source == 0),
+                    stop=(source == 1),
+                )
+
+        def copy_out_and_store(n):
+            nc.scalar.copy(out=shares[n][:, 0].rearrange("p h u d -> p (h u d)"), in_=summed[n][:])
+            store(n)
 
         transpose_x(0)
         regroup_w(0, 0, 0, nc.vector.tensor_copy)
@@ -218,6 +252,7 @@ def tile_multiscaleretention_pa_kernel(tc, x, sin, cos, Wq, Wk, out_0, out_1):
         transpose_x(3)
         project(1)
         make_q_factors(1)
+        projected = 2
         for n in range(TILES):
             g, j = divmod(n, ROW_TILES)
             if n % 2 == 0 and n + 4 < ROW_TILES:
@@ -228,11 +263,20 @@ def tile_multiscaleretention_pa_kernel(tc, x, sin, cos, Wq, Wk, out_0, out_1):
             if n == ROW_TILES + 2 * PASSES + 1:
                 make_k_factors()
             rotate(n)
-            if n + 2 < ROW_TILES:
-                quantise_x(n + 2)
-            if g + 1 < GROUPS and j >= ROW_TILES - 1 - PASSES and j < ROW_TILES - 1:
-                quantise_w_pass(g + 1, j - (ROW_TILES - 1 - PASSES))
-            if n + 2 < TILES:
-                project(n + 2)
-            if j + 1 == store_unit(n)[1]:
-                add_and_store(nc.vector if n >= TILES - UNIT_TILES else nc.gpsimd, n)
+            while projected < min(TILES, n + AHEAD + (0 if n < 2 else 1)):
+                if projected < ROW_TILES:
+                    quantise_x(projected)
+                project(projected)
+                projected += 1
+            if n <= VECTOR_ADDS and n >= UNIT_TILES and n % UNIT_TILES == 0:
+                add_and_store(nc.vector, n - 1)
+            if g + 1 < GROUPS and j == ROW_TILES - 1 - AHEAD:
+                quantise_w(g + 1)
+            if n >= TILES - UNIT_TILES:
+                add_and_store(nc.vector, n)
+            elif store_unit(n)[1] - store_unit(n)[0] == 1:
+                add_on_tensor(n)
+            elif n >= VECTOR_ADDS and j + 1 == store_unit(n)[1]:
+                add_and_store(nc.gpsimd, n)
+            if n - 2 in summed:
+                copy_out_and_store(n - 2)

@@ -143,7 +143,7 @@ def tile_multiscaleretention_pa_kernel(tc, x, sin, cos, Wq, Wk, out_0, out_1):
 
         def regroup_w(g, c, part, copy):
             if (c, part) == (0, 0):
-                w_grouped[g] = stage.tile([P, PASSES, GROUP_COLS, PACK], BF16, align_bytes=64, name="w_grouped", bufs=2)
+                w_grouped[g] = stage.tile([P, PASSES, GROUP_COLS, PACK], BF16, align_bytes=64, name="w_grouped", bufs=3)
             half = GROUP_COLS // 2
             cols = slice(part * half, (part + 1) * half)
             copy(
@@ -258,9 +258,10 @@ def tile_multiscaleretention_pa_kernel(tc, x, sin, cos, Wq, Wk, out_0, out_1):
             if n % 2 == 0 and n + 4 < ROW_TILES:
                 transpose_x(n + 4)
                 transpose_x(n + 5)
-            if g + 1 < GROUPS and 1 <= j <= 2 * PASSES:
-                regroup_w(g + 1, (j - 1) // 2, (j - 1) % 2, nc.scalar.copy)
-            if n == ROW_TILES + 2 * PASSES + 1:
+            if 1 <= n <= 2 * PASSES * (GROUPS - 1):
+                part = n - 1
+                regroup_w(1 + part // (2 * PASSES), part % (2 * PASSES) // 2, part % 2, nc.scalar.copy)
+            if n == 2 * PASSES * (GROUPS - 1) + 1:
                 make_k_factors()
             rotate(n)
             while projected < min(TILES, n + AHEAD + (0 if n < 2 else 1)):
@@ -270,7 +271,7 @@ def tile_multiscaleretention_pa_kernel(tc, x, sin, cos, Wq, Wk, out_0, out_1):
                 projected += 1
             if n <= VECTOR_ADDS and n >= UNIT_TILES and n % UNIT_TILES == 0:
                 add_and_store(nc.vector, n - 1)
-            if g + 1 < GROUPS and j == ROW_TILES - 1 - AHEAD:
+            if g + 1 < GROUPS and j == (4 if g == 0 else 3):
                 quantise_w(g + 1)
             if n >= TILES - UNIT_TILES:
                 add_and_store(nc.vector, n)

@@ -31,7 +31,8 @@ UNIT_TILES = 2
 UNITS = ((0, 2), (2, 3), (3, 5), (5, 6), (6, 8))
 AHEAD = 3
 VECTOR_ADDS = 4
-TABLE_PARTS = ((0, 2), (2, ROW_TILES))
+TABLE_PARTS = ((0, 2), (2, 4), (4, ROW_TILES))
+VECTOR_COLS = 320
 K_SCALE = CHANNELS**-0.5
 
 FLOPS = 2 * 2 * POSITIONS * K * HEADS * CHANNELS
@@ -79,33 +80,34 @@ def tile_multiscaleretention_pa_kernel(tc, x, sin, cos, Wq, Wk, out_0, out_1):
                     in_=rows[:, first * CHANNELS : last * CHANNELS],
                 )
 
-        load_x(0, 1)
         load_w(0, 0)
+        load_x(0, 1)
         load_w(0, 1)
-        load_tables(0)
         load_x(1, 2)
+        load_tables(0)
         load_x(2, 4)
         load_tables(1)
         load_x(4, 6)
-        load_w(1, 0)
+        load_tables(2)
         load_x(6, 8)
-        load_w(1, 1)
-        for g in range(2, GROUPS):
+        for g in range(1, GROUPS):
             for c in range(PASSES):
                 load_w(g, c)
 
         make_identity(nc, identity[:])
 
-        def make_q_factors(part):
-            first, last = TABLE_PARTS[part]
-            length = (last - first) * CHANNELS
-            sin_even = tables[part][:, length : 2 * length].rearrange("p (w z) -> p w z", z=2)[:, :, 0]
+        def make_q_factors(first):
+            last = first + UNIT_TILES
+            part, start, stop = [(n, a, b) for n, (a, b) in enumerate(TABLE_PARTS) if a <= first < b][0]
+            length = (stop - start) * CHANNELS
+            rows = slice((first - start) * CHANNELS, (last - start) * CHANNELS)
+            sin_even = tables[part][:, length : 2 * length][:, rows].rearrange("p (w z) -> p w z", z=2)[:, :, 0]
             nc.gpsimd.tensor_scalar(out=sin_even, in0=sin_even, scalar1=-1.0, scalar2=0.0, op0=MULT, op1=ADD)
             for source in range(2):
                 both = tables[part][:, source * length : source * length + 2 * (length + 1)].rearrange("p (e w) -> p e w", e=2)
                 nc.gpsimd.tensor_scalar(
                     out=factors[:, 0, first:last, source, :].rearrange("p j (i e) -> p j i e", e=2),
-                    in0=both[:, :, 0:length].rearrange("p e (j i z) -> p j i z e", i=PAIRS, z=2)[:, :, :, 0, :],
+                    in0=both[:, :, rows].rearrange("p e (j i z) -> p j i z e", i=PAIRS, z=2)[:, :, :, 0, :],
                     scalar1=1.0,
                     scalar2=0.0,
                     op0=MULT,
@@ -129,23 +131,30 @@ def tile_multiscaleretention_pa_kernel(tc, x, sin, cos, Wq, Wk, out_0, out_1):
                 for u in range(2):
                     first = c * (K_PASS // 2) + u
                     nc.tensor.transpose(turned[:, c, u, :], words[:, first : (c + 1) * (K_PASS // 2) : 2], identity[:])
-            grouped = stage.tile([P, PASSES * P * PACK], BF16, align_bytes=64, name="x_grouped", bufs=4)
+            pair, half = divmod(j, UNIT_TILES)
+            if half == 0:
+                x_grouped[pair] = stage.tile([P, UNIT_TILES, K], BF16, align_bytes=64, name="x_grouped%d" % pair, bufs=1)
             nc.scalar.copy(
-                out=grouped[:].bitcast(F32).rearrange("p (c r u) -> p c r u", c=PASSES, u=2),
+                out=x_grouped[pair][:, half].bitcast(F32).rearrange("p (c r u) -> p c r u", c=PASSES, u=2),
                 in_=turned[:].rearrange("p c u r -> p c r u"),
             )
-            x_grouped[j] = grouped
 
         def quantise_x(j):
-            nc.vector.quantize_mx(out=x_codes[:, j, :].bitcast(FP8X4), scales=x_scales[:, j, :], in_=x_grouped[j][:])
+            pair, half = divmod(j, UNIT_TILES)
+            nc.vector.quantize_mx(out=x_codes[:, j, :].bitcast(FP8X4), scales=x_scales[:, j, :], in_=x_grouped[pair][:, half])
+
+        def quantise_x_pair(j):
+            nc.vector.quantize_mx(
+                out=x_codes[:, j : j + UNIT_TILES, :].rearrange("p j w -> p (j w)").bitcast(FP8X4),
+                scales=x_scales[:, j : j + UNIT_TILES, :].rearrange("p j w -> p (j w)"),
+                in_=x_grouped[j // UNIT_TILES][:].rearrange("p j k -> p (j k)"),
+            )
 
         w_grouped = {}
 
-        def regroup_w(g, c, part, copy):
-            if (c, part) == (0, 0):
-                w_grouped[g] = stage.tile([P, PASSES, GROUP_COLS, PACK], BF16, align_bytes=64, name="w_grouped", bufs=3)
-            half = GROUP_COLS // 2
-            cols = slice(part * half, (part + 1) * half)
+        def regroup_w(g, c, cols, copy):
+            if g not in w_grouped:
+                w_grouped[g] = stage.tile([P, PASSES, GROUP_COLS, PACK], BF16, align_bytes=64, name="w_grouped%d" % g, bufs=1)
             copy(
                 out=w_grouped[g][:, c, cols, :].rearrange("p (n r) t -> p n t r", r=RUN),
                 in_=w_raw[g][:, c, :, cols].rearrange("p t (n r) -> p n t r", r=RUN),
@@ -187,10 +196,7 @@ def tile_multiscaleretention_pa_kernel(tc, x, sin, cos, Wq, Wk, out_0, out_1):
             j = n % ROW_TILES
             if n >= TILES - UNIT_TILES:
                 return j, j + 1
-            if n >= ROW_TILES:
-                return [unit for unit in UNITS if unit[0] <= j < unit[1]][0]
-            first = j - j % UNIT_TILES
-            return first, first + UNIT_TILES
+            return [unit for unit in UNITS if unit[0] <= j < unit[1]][0]
 
         shares = {}
 
@@ -210,14 +216,18 @@ def tile_multiscaleretention_pa_kernel(tc, x, sin, cos, Wq, Wk, out_0, out_1):
         def add_and_store(engine, n):
             j = n % ROW_TILES
             unit = shares[n - j + store_unit(n)[0]]
-            engine.tensor_tensor(out=unit[:, 0], in0=unit[:, 0], in1=unit[:, 1], op=ADD)
-            store(n)
+            summed_here = unit[:, 0]
+            if n in (1, 4, 12, 20):
+                name = "x_grouped3" if n == 1 else "w_grouped%d" % (n // ROW_TILES + 1)
+                summed_here = stage.tile([P, GROUP_HEADS, 2, CHANNELS], F32, align_bytes=64, name=name, bufs=1)
+            engine.tensor_tensor(out=summed_here[:], in0=unit[:, 0], in1=unit[:, 1], op=ADD)
+            store(n, summed_here)
 
-        def store(n):
+        def store(n, result):
             g, j = divmod(n, ROW_TILES)
             first, last = store_unit(n)
             heads = slice((g % 2) * GROUP_HEADS, (g % 2 + 1) * GROUP_HEADS)
-            nc.sync.dma_start(out=out_rows[g // 2][:, heads, first:last, :], in_=shares[n - j + first][:, 0])
+            nc.sync.dma_start(out=out_rows[g // 2][:, heads, first:last, :], in_=result[:])
 
         summed = {}
 
@@ -234,50 +244,65 @@ def tile_multiscaleretention_pa_kernel(tc, x, sin, cos, Wq, Wk, out_0, out_1):
 
         def copy_out_and_store(n):
             nc.scalar.copy(out=shares[n][:, 0].rearrange("p h u d -> p (h u d)"), in_=summed[n][:])
-            store(n)
+            store(n, shares[n][:, 0])
 
+        QX = {0: (2,), 1: (4,), 2: (6,)}
+        TX, KF, QW = 1, 9, (5, 4, 4)
+        projected, ready_groups = 2, 1
+        left, right = slice(0, VECTOR_COLS), slice(VECTOR_COLS, GROUP_COLS)
+        regroup_w(0, 0, left, nc.vector.tensor_copy)
+        regroup_w(0, 0, right, nc.scalar.copy)
         transpose_x(0)
-        regroup_w(0, 0, 0, nc.vector.tensor_copy)
-        regroup_w(0, 0, 1, nc.scalar.copy)
-        quantise_x(0)
-        regroup_w(0, 1, 0, nc.vector.tensor_copy)
-        regroup_w(0, 1, 1, nc.scalar.copy)
-        transpose_x(1)
         quantise_w_pass(0, 0)
-        quantise_w_pass(0, 1)
-        quantise_x(1)
+        regroup_w(0, 1, left, nc.vector.tensor_copy)
+        regroup_w(0, 1, right, nc.scalar.copy)
+        quantise_x(0)
+        transpose_x(1)
         make_q_factors(0)
+        quantise_w_pass(0, 1)
         project(0)
         transpose_x(2)
         transpose_x(3)
+        quantise_x(1)
         project(1)
-        make_q_factors(1)
-        projected = 2
+        make_q_factors(2)
+        transpose_x(4)
+        transpose_x(5)
+        transpose_x(6)
+        transpose_x(7)
+        make_q_factors(4)
+        make_q_factors(6)
+        quantised = 2
         for n in range(TILES):
             g, j = divmod(n, ROW_TILES)
-            if n % 2 == 0 and n + 4 < ROW_TILES:
-                transpose_x(n + 4)
-                transpose_x(n + 5)
-            if 1 <= n <= 2 * PASSES * (GROUPS - 1):
-                part = n - 1
-                regroup_w(1 + part // (2 * PASSES), part % (2 * PASSES) // 2, part % 2, nc.scalar.copy)
-            if n == 2 * PASSES * (GROUPS - 1) + 1:
+            if 1 <= n < 2 + 2 * PASSES * (GROUPS - 1) and n != KF:
+                part = n - 1 - (n > KF)
+                half = GROUP_COLS // 2
+                regroup_w(1 + part // (2 * PASSES), part % (2 * PASSES) // 2, slice(part % 2 * half, part % 2 * half + half), nc.scalar.copy)
+            if n == KF:
                 make_k_factors()
             rotate(n)
-            while projected < min(TILES, n + AHEAD + (0 if n < 2 else 1)):
-                if projected < ROW_TILES:
-                    quantise_x(projected)
+            if n in QX:
+                for t in QX[n]:
+                    quantise_x_pair(t)
+                    quantised += 2
+            if g + 1 < GROUPS and j == QW[g]:
+                quantise_w(g + 1)
+                ready_groups = g + 2
+            while projected < min(TILES, n + AHEAD + 1 + (n == 5), ROW_TILES * ready_groups) and (projected >= ROW_TILES or projected < quantised):
                 project(projected)
                 projected += 1
-            if n <= VECTOR_ADDS and n >= UNIT_TILES and n % UNIT_TILES == 0:
-                add_and_store(nc.vector, n - 1)
-            if g + 1 < GROUPS and j == (4 if g == 0 else 3):
-                quantise_w(g + 1)
+            if n == 2:
+                add_and_store(nc.gpsimd, 1)
+            if n == 5:
+                add_and_store(nc.gpsimd, 4)
             if n >= TILES - UNIT_TILES:
-                add_and_store(nc.vector, n)
+                if n == TILES - 1:
+                    add_and_store(nc.vector, n - 1)
+                    add_and_store(nc.vector, n)
             elif store_unit(n)[1] - store_unit(n)[0] == 1:
                 add_on_tensor(n)
-            elif n >= VECTOR_ADDS and j + 1 == store_unit(n)[1]:
+            elif n > 4 and j + 1 == store_unit(n)[1]:
                 add_and_store(nc.gpsimd, n)
             if n - 2 in summed:
                 copy_out_and_store(n - 2)

@@ -28,12 +28,25 @@ RUN = 4
 GROUPS = 2 * HEADS // GROUP_HEADS
 TILES = GROUPS * ROW_TILES
 UNIT_TILES = 2
-UNITS = ((0, 2), (2, 3), (3, 5), (5, 6), (6, 8))
 AHEAD = 3
-VECTOR_ADDS = 4
 TABLE_PARTS = ((0, 2), (2, 4), (4, ROW_TILES))
 VECTOR_COLS = 320
 K_SCALE = CHANNELS**-0.5
+T67 = 0
+VLAG = 2
+RG0 = 1
+KF = 8
+QX = {0: 2, 1: 4, 2: 6}
+QW = (5, 4, 4)
+MORE = (5,)
+SUM_IN = {1: "x_grouped3", 4: "w_grouped1", 12: "w_grouped2", 20: "w_grouped3"}
+DELAY = {1: 2, 4: 5}
+PLAN = (
+    ((0, 2, "G"), (2, 3, "T"), (3, 5, "G"), (5, 6, "T"), (6, 8, "G")),
+    ((0, 2, "G"), (2, 3, "T"), (3, 5, "G"), (5, 6, "T"), (6, 8, "G")),
+    ((0, 2, "G"), (2, 3, "T"), (3, 5, "G"), (5, 6, "T"), (6, 8, "G")),
+    ((0,2,"G"),(2,3,"T"),(3,5,"G"),(5,6,"V"),(6,7,"V"),(7,8,"V")),
+)
 
 FLOPS = 2 * 2 * POSITIONS * K * HEADS * CHANNELS
 
@@ -193,16 +206,14 @@ def tile_multiscaleretention_pa_kernel(tc, x, sin, cos, Wq, Wk, out_0, out_1):
             sums[n] = acc
 
         def store_unit(n):
-            j = n % ROW_TILES
-            if n >= TILES - UNIT_TILES:
-                return j, j + 1
-            return [unit for unit in UNITS if unit[0] <= j < unit[1]][0]
+            g, j = divmod(n, ROW_TILES)
+            return [unit for unit in PLAN[g] if unit[0] <= j < unit[1]][0]
 
         shares = {}
 
         def rotate(n):
             g, j = divmod(n, ROW_TILES)
-            first, last = store_unit(n)
+            first, last = store_unit(n)[:2]
             if j == first:
                 shares[n - j + first] = stage.tile([P, 2, GROUP_HEADS, last - first, CHANNELS], F32, name="shares", bufs=6)
             shape = [P, 2, GROUP_HEADS, PAIRS, 2]
@@ -217,15 +228,14 @@ def tile_multiscaleretention_pa_kernel(tc, x, sin, cos, Wq, Wk, out_0, out_1):
             j = n % ROW_TILES
             unit = shares[n - j + store_unit(n)[0]]
             summed_here = unit[:, 0]
-            if n in (1, 4, 12, 20):
-                name = "x_grouped3" if n == 1 else "w_grouped%d" % (n // ROW_TILES + 1)
-                summed_here = stage.tile([P, GROUP_HEADS, 2, CHANNELS], F32, align_bytes=64, name=name, bufs=1)
+            if n in SUM_IN:
+                summed_here = stage.tile([P, GROUP_HEADS, 2, CHANNELS], F32, align_bytes=64, name=SUM_IN[n], bufs=1)
             engine.tensor_tensor(out=summed_here[:], in0=unit[:, 0], in1=unit[:, 1], op=ADD)
             store(n, summed_here)
 
         def store(n, result):
             g, j = divmod(n, ROW_TILES)
-            first, last = store_unit(n)
+            first, last = store_unit(n)[:2]
             heads = slice((g % 2) * GROUP_HEADS, (g % 2 + 1) * GROUP_HEADS)
             nc.sync.dma_start(out=out_rows[g // 2][:, heads, first:last, :], in_=result[:])
 
@@ -246,9 +256,6 @@ def tile_multiscaleretention_pa_kernel(tc, x, sin, cos, Wq, Wk, out_0, out_1):
             nc.scalar.copy(out=shares[n][:, 0].rearrange("p h u d -> p (h u d)"), in_=summed[n][:])
             store(n, shares[n][:, 0])
 
-        QX = {0: (2,), 1: (4,), 2: (6,)}
-        TX, KF, QW = 1, 9, (5, 4, 4)
-        projected, ready_groups = 2, 1
         left, right = slice(0, VECTOR_COLS), slice(VECTOR_COLS, GROUP_COLS)
         regroup_w(0, 0, left, nc.vector.tensor_copy)
         regroup_w(0, 0, right, nc.scalar.copy)
@@ -268,41 +275,47 @@ def tile_multiscaleretention_pa_kernel(tc, x, sin, cos, Wq, Wk, out_0, out_1):
         make_q_factors(2)
         transpose_x(4)
         transpose_x(5)
-        transpose_x(6)
-        transpose_x(7)
+        if T67 == 0:
+            transpose_x(6)
+            transpose_x(7)
         make_q_factors(4)
         make_q_factors(6)
-        quantised = 2
+        projected, ready_groups, quantised = 2, 1, 2
+        late = []
         for n in range(TILES):
             g, j = divmod(n, ROW_TILES)
-            if 1 <= n < 2 + 2 * PASSES * (GROUPS - 1) and n != KF:
-                part = n - 1 - (n > KF)
-                half = GROUP_COLS // 2
-                regroup_w(1 + part // (2 * PASSES), part % (2 * PASSES) // 2, slice(part % 2 * half, part % 2 * half + half), nc.scalar.copy)
-            if n == KF:
-                make_k_factors()
+            if T67 and n == T67 - 1:
+                transpose_x(6)
+                transpose_x(7)
+            if n >= RG0 and n < RG0 + 13:
+                part = n - RG0
+                if part == KF:
+                    make_k_factors()
+                else:
+                    part = part - (part > KF)
+                    half = GROUP_COLS // 2
+                    regroup_w(1 + part // 4, part % 4 // 2, slice(part % 2 * half, part % 2 * half + half), nc.scalar.copy)
             rotate(n)
             if n in QX:
-                for t in QX[n]:
-                    quantise_x_pair(t)
-                    quantised += 2
+                quantise_x_pair(QX[n])
+                quantised += 2
             if g + 1 < GROUPS and j == QW[g]:
                 quantise_w(g + 1)
                 ready_groups = g + 2
-            while projected < min(TILES, n + AHEAD + 1 + (n == 5), ROW_TILES * ready_groups) and (projected >= ROW_TILES or projected < quantised):
+            while projected < min(TILES, n + AHEAD + 1 + (n in MORE), ROW_TILES * ready_groups) and (projected >= ROW_TILES or projected < quantised):
                 project(projected)
                 projected += 1
-            if n == 2:
-                add_and_store(nc.gpsimd, 1)
-            if n == 5:
-                add_and_store(nc.gpsimd, 4)
-            if n >= TILES - UNIT_TILES:
-                if n == TILES - 1:
-                    add_and_store(nc.vector, n - 1)
-                    add_and_store(nc.vector, n)
-            elif store_unit(n)[1] - store_unit(n)[0] == 1:
+            first, last, engine = store_unit(n)
+            if engine == "T":
                 add_on_tensor(n)
-            elif n > 4 and j + 1 == store_unit(n)[1]:
-                add_and_store(nc.gpsimd, n)
             if n - 2 in summed:
                 copy_out_and_store(n - 2)
+            if n in DELAY:
+                late.append(n)
+            elif engine == "G" and j + 1 == last:
+                add_and_store(nc.gpsimd, n)
+            for m in [m for m in late if DELAY[m] == n]:
+                add_and_store(nc.gpsimd, m)
+            for m in range(TILES):
+                if store_unit(m)[2] == "V" and m + 1 == m - m % ROW_TILES + store_unit(m)[1] and n == min(m + VLAG, TILES - 1):
+                    add_and_store(nc.vector, m)

@@ -22,60 +22,75 @@ PACK = 4
 K_PASS = P * PACK
 PASSES = K // K_PASS
 ROW_TILES = POSITIONS // P
+HALF_TILES = ROW_TILES // 2
+HALVES = 2
+HALF_COLS = HALF_TILES * P
 GROUP_HEADS = 4
 GROUP_COLS = GROUP_HEADS * CHANNELS
 RUN = 4
 GROUPS = 2 * HEADS // GROUP_HEADS
-TILES = GROUPS * ROW_TILES
 UNIT_TILES = 2
-AHEAD = 3
-TABLE_PARTS = ((0, 2), (2, 4), (4, ROW_TILES))
-VECTOR_COLS = 320
 K_SCALE = CHANNELS**-0.5
-T67 = 0
-VLAG = 2
-RG0 = 1
-KF = 8
-QX = {0: 2, 1: 4, 2: 6}
-QW = (5, 4, 4)
-MORE = (5,)
-SUM_IN = {1: "x_grouped3", 4: "w_grouped1", 12: "w_grouped2", 20: "w_grouped3"}
-DELAY = {1: 2, 4: 5}
-PLAN = (
-    ((0, 2, "G"), (2, 3, "T"), (3, 5, "G"), (5, 6, "T"), (6, 8, "G")),
-    ((0, 2, "G"), (2, 3, "T"), (3, 5, "G"), (5, 6, "T"), (6, 8, "G")),
-    ((0, 2, "G"), (2, 3, "T"), (3, 5, "G"), (5, 6, "T"), (6, 8, "G")),
-    ((0,2,"G"),(2,3,"T"),(3,5,"G"),(5,6,"V"),(6,7,"V"),(7,8,"V")),
-)
+VECTOR_COLS = 320
+LOADS = (('w', 0, 0), ('x', 0, 1), ('w', 0, 1), ('t', 0), ('x', 1, 2), ('x', 2, 4), ('t', 1), ('x', 4, 6), ('x', 6, 8), ('u', 1), ('u', 0), ('w', 1, 0), ('w', 1, 1), ('w', 2, 0), ('w', 2, 1), ('w', 3, 0), ('w', 3, 1))
+SEQ = [('o', 0, 0), ('o', 0, 1), ('o', 0, 2), ('o', 0, 3), ('n', 0, 0), ('n', 0, 1), ('n', 0, 2), ('n', 0, 3), ('o', 1, 0), ('n', 1, 0), ('o', 1, 1), ('n', 1, 1), ('o', 1, 2), ('n', 1, 2), ('n', 1, 3), ('o', 1, 3), ('n', 2, 0), ('n', 2, 1), ('o', 2, 0), ('o', 2, 1), ('n', 2, 2), ('n', 2, 3), ('o', 2, 2), ('o', 2, 3), ('o', 3, 0), ('n', 3, 0), ('n', 3, 1), ('o', 3, 1), ('n', 3, 2), ('n', 3, 3), ('o', 3, 2), ('o', 3, 3)]
+ACC = 5
+BACK = 3
+LEAD = 2
+BLAG = 1
+CLAG = 2
+BATCH = 2
+QUNITS = (((0, 2), (2, 4)), ((0, 2), (2, 4)), ((0, 2), (2, 4)), ((0, 1), (1, 2), (2, 3), (3, 4)))
+VADD = ((3, 2), (3, 3))
+F_SET = (8, 10, 12, 18, 19, 22)
+KBUFS = 4
+QBUFS = 5
+HEAD = (('rg', 0, 0, 0, 384, 'V'), ('rg', 0, 0, 384, 512, 'S'), ('tx', 0), ('qp', 0, 0), ('rg', 0, 1, 0, 384, 'V'), ('rg', 0, 1, 384, 512, 'S'), ('ql', 0, 1), ('tx', 1), ('mf', 0, 'S'), ('qp', 0, 1), ('pj', 0), ('tx', 2), ('tx', 3), ('ql', 1, 2), ('pj', 1), ('mf', 1, 'G'), ('ss', 'G'), ('tx', 4), ('tx', 5))
+PROJECTED = 2
+BEFORE = {1: (('nf', 0), ('nf', 1), ('rg', 1, 0, 256, 512, 'S')), 2: (('rg', 1, 0, 0, 256, 'G'), ('rg', 1, 1, 0, 256, 'S')), 3: (('rg', 1, 1, 256, 512, 'S'), ('rg', 2, 0, 0, 256, 'S')), 4: (('rg', 2, 0, 256, 512, 'S'),), 5: (('rg', 2, 1, 0, 256, 'S'),), 6: (('rg', 2, 1, 256, 512, 'S'),), 12: (('rg', 3, 0, 0, 256, 'S'), ('sf',)), 13: (('rg', 3, 0, 256, 512, 'S'),), 14: (('rg', 3, 1, 0, 256, 'S'),), 15: (('rg', 3, 1, 256, 512, 'S'),)}
+AFTER = {0: (('ql', 2, 4), ('tx', 6), ('tx', 7)), 2: (('qh', 0, 2),), 7: (('qw', 1),), 8: (('qw', 2),), 18: (('qw', 3),)}
+SYNC = {(0, 0): 'hi_grouped', (1, 2): 'w_grouped2'}
+GDELAY = {(0, 1): 2}
+NQ = 0
+LIMIT = {0: 4, 1: 4, 2: 8, 3: 8, 4: 8, 5: 8, 6: 8, 7: 16, 8: 24, 9: 24, 10: 24, 11: 24, 12: 24, 13: 24, 14: 24, 15: 24, 16: 24, 17: 24, 18: 32, 19: 32, 20: 32, 21: 32, 22: 32, 23: 32, 24: 32, 25: 32, 26: 32, 27: 32, 28: 32, 29: 32, 30: 32, 31: 32}
 
 FLOPS = 2 * 2 * POSITIONS * K * HEADS * CHANNELS
 
 
 def tile_multiscaleretention_pa_kernel(tc, x, sin, cos, Wq, Wk, out_0, out_1):
     nc = tc.nc
-
     x_rows = x.flatten_outer_dims().rearrange("(p j) k -> p j k", j=ROW_TILES)
     cos_rows = cos.rearrange("(p j) d -> p (j d)", j=ROW_TILES)
     sin_rows = sin.rearrange("(p j) d -> p (j d)", j=ROW_TILES)
-    out_rows = [o.rearrange("b h (p j) d -> p (b h) j d", j=ROW_TILES) for o in (out_0, out_1)]
+    o_rows = [o.rearrange("b h (p j) d -> p (b h) j d", j=ROW_TILES) for o in (out_0, out_1)]
+    n_rows = [o.rearrange("b h (p f j) d -> p (b h) f (j d)", f=HALVES, j=HALF_TILES) for o in (out_0, out_1)]
     w_rows = [w.rearrange("(c p t) n -> p c t n", c=PASSES, t=PACK) for w in (Wq, Wk)]
 
     with ExitStack() as ctx:
         keep = ctx.enter_context(tc.tile_pool(name="keep", bufs=1))
         stage = ctx.enter_context(tc.tile_pool(name="stage", bufs=3))
-        psum_t = ctx.enter_context(tc.psum_pool(name="psum_t", bufs=2))
-        psum_acc = ctx.enter_context(tc.psum_pool(name="psum_acc", bufs=6))
+        psum_acc = ctx.enter_context(tc.psum_pool(name="psum_acc", bufs=ACC))
+        psum_back = ctx.enter_context(tc.psum_pool(name="psum_back", bufs=BACK))
         ctx.enter_context(tc.manual_schedule())
 
         x_sb = keep.tile([P, ROW_TILES, K], BF16)
-        tables = [keep.tile([P, 3 * (last - first) * CHANNELS + 2], BF16, name="tables%d" % first) for first, last in TABLE_PARTS]
+        tables = [keep.tile([P, 3 * UNIT_TILES * CHANNELS + 2], BF16, name="tables%d" % n) for n in range(HALF_TILES // UNIT_TILES)]
+        upper = [keep.tile([P, HALF_TILES, CHANNELS], BF16, name="upper%d" % s) for s in range(2)]
         w_raw = [keep.tile([P, PASSES, PACK, GROUP_COLS], BF16, name="w_raw%d" % g) for g in range(GROUPS)]
-        x_codes = keep.tile([P, ROW_TILES, PASSES * P], U32, align_bytes=64)
-        x_scales = keep.tile([P, ROW_TILES, PASSES * P], U8, align_bytes=64)
+        lo_codes = keep.tile([P, HALF_TILES, PASSES, P], U32, align_bytes=64)
+        lo_scales = keep.tile([P, HALF_TILES, PASSES, P], U8, align_bytes=64)
+        hi_codes = keep.tile([P, PASSES, HALF_COLS], U32, align_bytes=64)
+        hi_scales = keep.tile([P, PASSES, HALF_COLS], U8, align_bytes=64)
         w_codes = keep.tile([P, GROUPS, PASSES, GROUP_COLS], U32, align_bytes=64)
         w_scales = keep.tile([P, GROUPS, PASSES, GROUP_COLS], U8, align_bytes=64)
-        factors = keep.tile([P, 2, ROW_TILES, 2, CHANNELS], F32)
+        factors = keep.tile([P, 2, HALF_TILES, 2, CHANNELS], F32)
+        n_factors = keep.tile([P, 2, HALF_COLS], F32)
+        partner_sin = keep.tile([P, HALF_TILES, CHANNELS], BF16)
         identity = keep.tile([P, P], F32)
+        swap = keep.tile([P, P], F32)
+        identity_bf = keep.tile([P, P], BF16)
+        w_grouped = {}
+        half = GROUP_COLS // 2
 
         def load_x(first, last):
             nc.sync.dma_start(out=x_sb[:, first:last, :], in_=x_rows[:, first:last, :])
@@ -85,49 +100,46 @@ def tile_multiscaleretention_pa_kernel(tc, x, sin, cos, Wq, Wk, out_0, out_1):
             nc.sync.dma_start(out=w_raw[g][:, c, :, :], in_=w_rows[g // 2][:, c, :, cols])
 
         def load_tables(part):
-            first, last = TABLE_PARTS[part]
-            length = (last - first) * CHANNELS
-            for place, rows in enumerate((cos_rows, sin_rows, cos_rows)):
+            first, last = part * UNIT_TILES, (part + 1) * UNIT_TILES
+            length = UNIT_TILES * CHANNELS
+            for spot, rows in enumerate((cos_rows, sin_rows, cos_rows)):
                 nc.sync.dma_start(
-                    out=tables[part][:, place * length : (place + 1) * length],
+                    out=tables[part][:, spot * length : (spot + 1) * length],
                     in_=rows[:, first * CHANNELS : last * CHANNELS],
                 )
 
-        load_w(0, 0)
-        load_x(0, 1)
-        load_w(0, 1)
-        load_x(1, 2)
-        load_tables(0)
-        load_x(2, 4)
-        load_tables(1)
-        load_x(4, 6)
-        load_tables(2)
-        load_x(6, 8)
-        for g in range(1, GROUPS):
-            for c in range(PASSES):
-                load_w(g, c)
+        def load_upper(s):
+            nc.sync.dma_start(
+                out=upper[s][:].rearrange("p j d -> p (j d)"),
+                in_=(cos_rows, sin_rows)[s][:, HALF_TILES * CHANNELS : ROW_TILES * CHANNELS],
+            )
+
+        for what in LOADS:
+            {"x": load_x, "w": load_w, "t": load_tables, "u": load_upper}[what[0]](*what[1:])
 
         make_identity(nc, identity[:])
+        nc.vector.tensor_copy(out=swap[:, 0:P:2], in_=identity[:, 1:P:2])
+        nc.vector.tensor_copy(out=swap[:, 1:P:2], in_=identity[:, 0:P:2])
+        nc.vector.tensor_copy(out=identity_bf[:], in_=identity[:])
 
-        def make_q_factors(first):
-            last = first + UNIT_TILES
-            part, start, stop = [(n, a, b) for n, (a, b) in enumerate(TABLE_PARTS) if a <= first < b][0]
-            length = (stop - start) * CHANNELS
-            rows = slice((first - start) * CHANNELS, (last - start) * CHANNELS)
-            sin_even = tables[part][:, length : 2 * length][:, rows].rearrange("p (w z) -> p w z", z=2)[:, :, 0]
-            nc.gpsimd.tensor_scalar(out=sin_even, in0=sin_even, scalar1=-1.0, scalar2=0.0, op0=MULT, op1=ADD)
+        def make_factors(part, engine):
+            first, last = part * UNIT_TILES, (part + 1) * UNIT_TILES
+            length = UNIT_TILES * CHANNELS
+            sin_even = tables[part][:, length : 2 * length].rearrange("p (w z) -> p w z", z=2)[:, :, 0]
+            if engine == "G":
+                nc.gpsimd.tensor_scalar(out=sin_even, in0=sin_even, scalar1=-1.0, scalar2=0.0, op0=MULT, op1=ADD)
+            else:
+                nc.scalar.activation(out=sin_even, in_=sin_even, func=COPY, scale=-1.0)
             for source in range(2):
                 both = tables[part][:, source * length : source * length + 2 * (length + 1)].rearrange("p (e w) -> p e w", e=2)
-                nc.gpsimd.tensor_scalar(
-                    out=factors[:, 0, first:last, source, :].rearrange("p j (i e) -> p j i e", e=2),
-                    in0=both[:, :, rows].rearrange("p e (j i z) -> p j i z e", i=PAIRS, z=2)[:, :, :, 0, :],
-                    scalar1=1.0,
-                    scalar2=0.0,
-                    op0=MULT,
-                    op1=ADD,
-                )
+                o = factors[:, 0, first:last, source, :].rearrange("p j (i e) -> p j i e", e=2)
+                i = both[:, :, 0:length].rearrange("p e (j i z) -> p j i z e", i=PAIRS, z=2)[:, :, :, 0, :]
+                if engine == "G":
+                    nc.gpsimd.tensor_scalar(out=o, in0=i, scalar1=1.0, scalar2=0.0, op0=MULT, op1=ADD)
+                else:
+                    nc.scalar.copy(out=o, in_=i)
 
-        def make_k_factors():
+        def scale_factors():
             nc.scalar.activation(
                 out=factors[:, 1].rearrange("p j s d -> p (j s d)"),
                 in_=factors[:, 0].rearrange("p j s d -> p (j s d)"),
@@ -135,43 +147,70 @@ def tile_multiscaleretention_pa_kernel(tc, x, sin, cos, Wq, Wk, out_0, out_1):
                 scale=K_SCALE,
             )
 
+        def swap_sin(engine):
+            for e in range(2):
+                o, i, f = partner_sin[:, :, e::2], upper[1][:, :, 1 - e :: 2], 1.0 - 2.0 * e
+                if engine == "G":
+                    nc.gpsimd.tensor_scalar(out=o, in0=i, scalar1=f, scalar2=0.0, op0=MULT, op1=ADD)
+                elif engine == "V":
+                    nc.vector.tensor_scalar(out=o, in0=i, scalar1=f, scalar2=0.0, op0=MULT, op1=ADD)
+                else:
+                    nc.scalar.activation(out=o, in_=i, func=COPY, scale=f)
+
+        def make_n_factors(s):
+            turned = psum_back.tile([P, HALF_TILES, P], BF16, name="back")
+            for jj in range(HALF_TILES):
+                nc.tensor.transpose(turned[:, jj, :], (partner_sin if s else upper[0])[:, jj, :], identity_bf[:])
+            nc.scalar.copy(out=n_factors[:, s, :], in_=turned[:].rearrange("p j r -> p (j r)"))
+
         x_grouped = {}
 
         def transpose_x(j):
             words = x_sb[:, j, :].bitcast(F32)
-            turned = psum_t.tile([P, PASSES, 2, P], F32, name="turned")
+            turned = psum_back.tile([P, PASSES, 2, P], F32, name="back")
             for c in range(PASSES):
                 for u in range(2):
                     first = c * (K_PASS // 2) + u
                     nc.tensor.transpose(turned[:, c, u, :], words[:, first : (c + 1) * (K_PASS // 2) : 2], identity[:])
-            pair, half = divmod(j, UNIT_TILES)
-            if half == 0:
-                x_grouped[pair] = stage.tile([P, UNIT_TILES, K], BF16, align_bytes=64, name="x_grouped%d" % pair, bufs=1)
-            nc.scalar.copy(
-                out=x_grouped[pair][:, half].bitcast(F32).rearrange("p (c r u) -> p c r u", c=PASSES, u=2),
-                in_=turned[:].rearrange("p c u r -> p c r u"),
-            )
+            if j < HALF_TILES:
+                pair, jj = divmod(j, UNIT_TILES)
+                if jj == 0:
+                    x_grouped[pair] = stage.tile([P, UNIT_TILES, K], BF16, align_bytes=64, name="lo_grouped%d" % pair, bufs=1)
+                out = x_grouped[pair][:, jj].bitcast(F32).rearrange("p (c r u) -> p c r u", c=PASSES, u=2)
+            else:
+                if j == HALF_TILES:
+                    x_grouped[2] = stage.tile([P, PASSES, HALF_TILES, P * PACK], BF16, align_bytes=64, name="hi_grouped", bufs=1)
+                out = x_grouped[2][:, :, j - HALF_TILES, :].bitcast(F32).rearrange("p c (r u) -> p c r u", u=2)
+            nc.scalar.copy(out=out, in_=turned[:].rearrange("p c u r -> p c r u"))
 
-        def quantise_x(j):
-            pair, half = divmod(j, UNIT_TILES)
-            nc.vector.quantize_mx(out=x_codes[:, j, :].bitcast(FP8X4), scales=x_scales[:, j, :], in_=x_grouped[pair][:, half])
-
-        def quantise_x_pair(j):
+        def quantise_lo(first, last):
+            pair = first // UNIT_TILES
             nc.vector.quantize_mx(
-                out=x_codes[:, j : j + UNIT_TILES, :].rearrange("p j w -> p (j w)").bitcast(FP8X4),
-                scales=x_scales[:, j : j + UNIT_TILES, :].rearrange("p j w -> p (j w)"),
-                in_=x_grouped[j // UNIT_TILES][:].rearrange("p j k -> p (j k)"),
+                out=lo_codes[:, first:last].rearrange("p j c r -> p (j c r)").bitcast(FP8X4),
+                scales=lo_scales[:, first:last].rearrange("p j c r -> p (j c r)"),
+                in_=x_grouped[pair][:, first - pair * UNIT_TILES : last - pair * UNIT_TILES].rearrange("p j k -> p (j k)"),
             )
 
-        w_grouped = {}
+        def quantise_hi(first, last):
+            nc.vector.quantize_mx(
+                out=hi_codes[:, first:last].rearrange("p c r -> p (c r)").bitcast(FP8X4),
+                scales=hi_scales[:, first:last].rearrange("p c r -> p (c r)"),
+                in_=x_grouped[2][:, first:last].rearrange("p c j k -> p (c j k)"),
+            )
 
-        def regroup_w(g, c, cols, copy):
+        def regroup_w(g, c, first, last, engine):
             if g not in w_grouped:
                 w_grouped[g] = stage.tile([P, PASSES, GROUP_COLS, PACK], BF16, align_bytes=64, name="w_grouped%d" % g, bufs=1)
-            copy(
-                out=w_grouped[g][:, c, cols, :].rearrange("p (n r) t -> p n t r", r=RUN),
-                in_=w_raw[g][:, c, :, cols].rearrange("p t (n r) -> p n t r", r=RUN),
-            )
+            cols = slice(first, last)
+            out, src = w_grouped[g][:, c, cols, :], w_raw[g][:, c, :, cols]
+            if engine == "G":
+                nc.gpsimd.tensor_scalar(
+                    out=out, in0=src.rearrange("p t n -> p n t"), scalar1=1.0, scalar2=0.0, op0=MULT, op1=ADD
+                )
+            else:
+                (nc.vector.tensor_copy if engine == "V" else nc.scalar.copy)(
+                    out=out.rearrange("p (n r) t -> p n t r", r=RUN), in_=src.rearrange("p t (n r) -> p n t r", r=RUN)
+                )
 
         def quantise_w(g):
             nc.vector.quantize_mx(
@@ -190,132 +229,145 @@ def tile_multiscaleretention_pa_kernel(tc, x, sin, cos, Wq, Wk, out_0, out_1):
         sums = {}
 
         def project(n):
-            g, j = divmod(n, ROW_TILES)
-            acc = psum_acc.tile([P, GROUP_COLS], F32)
+            item = SEQ[n]
+            acc = psum_acc.tile([P, GROUP_COLS], F32, name="acc")
             for c in range(PASSES):
-                rows = slice(c * P, (c + 1) * P)
+                if item[0] == "o":
+                    g, j = item[1:]
+                    ops = (lo_codes[:, j, c, :], lo_scales[:, j, c, :], w_codes[:, g, c, :], w_scales[:, g, c, :])
+                else:
+                    g, h = item[1:]
+                    rows = slice(h * CHANNELS, (h + 1) * CHANNELS)
+                    ops = (w_codes[:, g, c, rows], w_scales[:, g, c, rows], hi_codes[:, c, :], hi_scales[:, c, :])
                 nc.tensor.matmul_mx(
                     out=acc[:],
-                    lhsT=x_codes[:, j, rows].bitcast(FP8X4),
-                    lhsT_scale=x_scales[:, j, rows],
-                    rhs=w_codes[:, g, c, :].bitcast(FP8X4),
-                    rhs_scale=w_scales[:, g, c, :],
+                    lhsT=ops[0].bitcast(FP8X4),
+                    lhsT_scale=ops[1],
+                    rhs=ops[2].bitcast(FP8X4),
+                    rhs_scale=ops[3],
                     start=(c == 0),
                     stop=(c == PASSES - 1),
                 )
             sums[n] = acc
 
-        def store_unit(n):
-            g, j = divmod(n, ROW_TILES)
-            return [unit for unit in PLAN[g] if unit[0] <= j < unit[1]][0]
-
         shares = {}
+        q_units = {}
 
-        def rotate(n):
-            g, j = divmod(n, ROW_TILES)
-            first, last = store_unit(n)[:2]
-            if j == first:
-                shares[n - j + first] = stage.tile([P, 2, GROUP_HEADS, last - first, CHANNELS], F32, name="shares", bufs=6)
+        def unit_of(j, g):
+            for a, b in QUNITS[g]:
+                if a <= j < b:
+                    return a, b
+
+        def multiply(n):
+            item = SEQ[n]
+            if item[0] == "n":
+                shares[n] = stage.tile([P, 2, HALF_COLS], F32, name="shares", bufs=KBUFS)
+                if n in F_SET:
+                    nc.vector.tensor_tensor(out=shares[n][:, 0, :], in0=sums[n][:], in1=n_factors[:, 0, :], op=MULT)
+                    lifted = stage.tile([P, HALF_COLS], F32, name="lifted", bufs=2)
+                    nc.scalar.copy(out=lifted[:], in_=sums[n][:])
+                    nc.gpsimd.tensor_tensor(out=shares[n][:, 1, :], in0=lifted[:], in1=n_factors[:, 1, :], op=MULT)
+                    return
+                nc.vector.tensor_tensor(
+                    out=shares[n][:],
+                    in0=sums[n][:].unsqueeze(1).to_broadcast([P, 2, HALF_COLS]),
+                    in1=n_factors[:],
+                    op=MULT,
+                )
+                return
+            g, j = item[1:]
+            a, b = unit_of(j, g)
+            if j == a:
+                q_units[g, a] = stage.tile([P, 2, GROUP_HEADS, b - a, CHANNELS], F32, name="q_units", bufs=QBUFS)
+            unit = q_units[g, a]
+            if n in F_SET:
+                shape = [P, GROUP_HEADS, PAIRS, 2]
+                nc.vector.tensor_tensor(
+                    out=unit[:, 0, :, j - a, :].rearrange("p h (i e) -> p h i e", e=2),
+                    in0=sums[n][:].rearrange("p (h i s) -> p s h i", h=GROUP_HEADS, s=2)[:, 0].unsqueeze(3).to_broadcast(shape),
+                    in1=factors[:, g // 2, j, 0].rearrange("p (i e) -> p i e", e=2).unsqueeze(1).to_broadcast(shape),
+                    op=MULT,
+                )
+                odd = stage.tile([P, GROUP_COLS // 2], F32, name="odd", bufs=3)
+                nc.scalar.copy(out=odd[:], in_=sums[n][:, 1::2])
+                nc.gpsimd.tensor_tensor(
+                    out=unit[:, 1, :, j - a, :].rearrange("p h (i e) -> p h i e", e=2),
+                    in0=odd[:].rearrange("p (h i) -> p h i", h=GROUP_HEADS).unsqueeze(3).to_broadcast(shape),
+                    in1=factors[:, g // 2, j, 1].rearrange("p (i e) -> p i e", e=2).unsqueeze(1).to_broadcast(shape),
+                    op=MULT,
+                )
+                return
             shape = [P, 2, GROUP_HEADS, PAIRS, 2]
             nc.vector.tensor_tensor(
-                out=shares[n - j + first][:, :, :, j - first, :].rearrange("p s h (i e) -> p s h i e", e=2),
+                out=unit[:, :, :, j - a, :].rearrange("p s h (i e) -> p s h i e", e=2),
                 in0=sums[n][:].rearrange("p (h i s) -> p s h i", h=GROUP_HEADS, s=2).unsqueeze(4).to_broadcast(shape),
                 in1=factors[:, g // 2, j].rearrange("p s (i e) -> p s i e", e=2).unsqueeze(2).to_broadcast(shape),
                 op=MULT,
             )
 
-        def add_and_store(engine, n):
-            j = n % ROW_TILES
-            unit = shares[n - j + store_unit(n)[0]]
-            summed_here = unit[:, 0]
-            if n in SUM_IN:
-                summed_here = stage.tile([P, GROUP_HEADS, 2, CHANNELS], F32, align_bytes=64, name=SUM_IN[n], bufs=1)
-            engine.tensor_tensor(out=summed_here[:], in0=unit[:, 0], in1=unit[:, 1], op=ADD)
-            store(n, summed_here)
+        def add_q(n):
+            g, j = SEQ[n][1:]
+            a, b = unit_of(j, g)
+            unit = q_units[g, a]
+            result = unit[:, 0]
+            if (g, a) in SYNC:
+                result = stage.tile([P, GROUP_HEADS, b - a, CHANNELS], F32, align_bytes=64, name=SYNC[g, a], bufs=1)
+            engine = nc.vector if (g, a) in VADD else nc.gpsimd
+            engine.tensor_tensor(out=result[:], in0=unit[:, 0], in1=unit[:, 1], op=ADD)
+            nc.sync.dma_start(out=o_rows[g // 2][:, g % 2 * GROUP_HEADS : (g % 2 + 1) * GROUP_HEADS, a:b, :], in_=result[:])
 
-        def store(n, result):
-            g, j = divmod(n, ROW_TILES)
-            first, last = store_unit(n)[:2]
-            heads = slice((g % 2) * GROUP_HEADS, (g % 2 + 1) * GROUP_HEADS)
-            nc.sync.dma_start(out=out_rows[g // 2][:, heads, first:last, :], in_=result[:])
+        backs = {}
 
-        summed = {}
+        def turn_back(n):
+            back = psum_back.tile([P, HALF_TILES, CHANNELS], F32, name="back")
+            for jj in range(HALF_TILES):
+                cols = slice(jj * P, (jj + 1) * P)
+                nc.tensor.matmul(out=back[:, jj, :], lhsT=shares[n][:, 0, cols], rhs=identity[:], is_transpose=True, start=True, stop=False)
+                nc.tensor.matmul(out=back[:, jj, :], lhsT=shares[n][:, 1, cols], rhs=swap[:], is_transpose=True, start=False, stop=True)
+            backs[n] = back
 
-        def add_on_tensor(n):
-            summed[n] = psum_t.tile([P, GROUP_COLS], F32, name="turned")
-            for source in range(2):
-                nc.tensor.matmul(
-                    out=summed[n][:],
-                    lhsT=identity[:],
-                    rhs=shares[n][:, source].rearrange("p h u d -> p (h u d)"),
-                    start=(source == 0),
-                    stop=(source == 1),
-                )
+        def copy_back(n):
+            g, h = SEQ[n][1:]
+            result = stage.tile([P, HALF_TILES * CHANNELS], F32, name="result", bufs=4)
+            flat = backs[n][:].rearrange("p j d -> p (j d)")
+            if g < 2:
+                nc.scalar.copy(out=result[:], in_=flat)
+            else:
+                nc.scalar.activation(out=result[:], in_=flat, func=COPY, scale=K_SCALE)
+            (nc.scalar if NQ else nc.sync).dma_start(out=n_rows[g // 2][:, g % 2 * GROUP_HEADS + h, 1, :], in_=result[:])
 
-        def copy_out_and_store(n):
-            nc.scalar.copy(out=shares[n][:, 0].rearrange("p h u d -> p (h u d)"), in_=summed[n][:])
-            store(n, shares[n][:, 0])
+        ops = {
+            "rg": regroup_w, "tx": transpose_x, "ql": quantise_lo, "qh": quantise_hi, "qw": quantise_w, "qp": quantise_w_pass, "mf": make_factors,
+            "sf": scale_factors, "ss": swap_sin, "nf": make_n_factors, "pj": project,
+        }
 
-        left, right = slice(0, VECTOR_COLS), slice(VECTOR_COLS, GROUP_COLS)
-        regroup_w(0, 0, left, nc.vector.tensor_copy)
-        regroup_w(0, 0, right, nc.scalar.copy)
-        transpose_x(0)
-        quantise_w_pass(0, 0)
-        regroup_w(0, 1, left, nc.vector.tensor_copy)
-        regroup_w(0, 1, right, nc.scalar.copy)
-        quantise_x(0)
-        transpose_x(1)
-        make_q_factors(0)
-        quantise_w_pass(0, 1)
-        project(0)
-        transpose_x(2)
-        transpose_x(3)
-        quantise_x(1)
-        project(1)
-        make_q_factors(2)
-        transpose_x(4)
-        transpose_x(5)
-        if T67 == 0:
-            transpose_x(6)
-            transpose_x(7)
-        make_q_factors(4)
-        make_q_factors(6)
-        projected, ready_groups, quantised = 2, 1, 2
-        late = []
-        for n in range(TILES):
-            g, j = divmod(n, ROW_TILES)
-            if T67 and n == T67 - 1:
-                transpose_x(6)
-                transpose_x(7)
-            if n >= RG0 and n < RG0 + 13:
-                part = n - RG0
-                if part == KF:
-                    make_k_factors()
-                else:
-                    part = part - (part > KF)
-                    half = GROUP_COLS // 2
-                    regroup_w(1 + part // 4, part % 4 // 2, slice(part % 2 * half, part % 2 * half + half), nc.scalar.copy)
-            rotate(n)
-            if n in QX:
-                quantise_x_pair(QX[n])
-                quantised += 2
-            if g + 1 < GROUPS and j == QW[g]:
-                quantise_w(g + 1)
-                ready_groups = g + 2
-            while projected < min(TILES, n + AHEAD + 1 + (n in MORE), ROW_TILES * ready_groups) and (projected >= ROW_TILES or projected < quantised):
+        def run(todo):
+            for op in todo:
+                ops[op[0]](*op[1:])
+
+        done, late = [], []
+        run(HEAD)
+        projected = PROJECTED
+        for n in range(len(SEQ)):
+            run(BEFORE.get(n, ()))
+            multiply(n)
+            run(AFTER.get(n, ()))
+            while projected < min(len(SEQ), n + LEAD + 1) and projected < LIMIT.get(n, 99):
                 project(projected)
                 projected += 1
-            first, last, engine = store_unit(n)
-            if engine == "T":
-                add_on_tensor(n)
-            if n - 2 in summed:
-                copy_out_and_store(n - 2)
-            if n in DELAY:
-                late.append(n)
-            elif engine == "G" and j + 1 == last:
-                add_and_store(nc.gpsimd, n)
-            for m in [m for m in late if DELAY[m] == n]:
-                add_and_store(nc.gpsimd, m)
-            for m in range(TILES):
-                if store_unit(m)[2] == "V" and m + 1 == m - m % ROW_TILES + store_unit(m)[1] and n == min(m + VLAG, TILES - 1):
-                    add_and_store(nc.vector, m)
+            waiting = [m for m in range(n + 1) if SEQ[m][0] == "n" and m not in backs and m <= n - BLAG]
+            if len(waiting) >= BATCH or n == len(SEQ) - 1 or (waiting and max(m for m in range(len(SEQ)) if SEQ[m][0] == "n") <= n):
+                for m in [m for m in range(n + 1) if SEQ[m][0] == "n" and m not in backs] if n == len(SEQ) - 1 else waiting:
+                    turn_back(m)
+            for m in sorted(backs):
+                if m not in done and (m <= n - CLAG or n == len(SEQ) - 1):
+                    copy_back(m)
+                    done.append(m)
+            if SEQ[n][0] == "o":
+                g, j = SEQ[n][1:]
+                if j + 1 == unit_of(j, g)[1]:
+                    late.append(n)
+            for m in late[:]:
+                if GDELAY.get(SEQ[m][1:], m) <= n:
+                    add_q(m)
+                    late.remove(m)

@@ -32,27 +32,27 @@ GROUPS = 2 * HEADS // GROUP_HEADS
 UNIT_TILES = 2
 K_SCALE = CHANNELS**-0.5
 VECTOR_COLS = 320
-LOADS = (('w', 0, 0), ('x', 0, 1), ('w', 0, 1), ('t', 0), ('x', 1, 2), ('x', 2, 4), ('t', 1), ('x', 4, 6), ('x', 6, 8), ('u', 1), ('u', 0), ('w', 1, 0), ('w', 1, 1), ('w', 2, 0), ('w', 2, 1), ('w', 3, 0), ('w', 3, 1))
-SEQ = [('o', 0, 0), ('o', 0, 1), ('o', 0, 2), ('o', 0, 3), ('n', 0, 0), ('n', 0, 1), ('n', 0, 2), ('n', 0, 3), ('o', 1, 0), ('n', 1, 0), ('o', 1, 1), ('n', 1, 1), ('o', 1, 2), ('n', 1, 2), ('n', 1, 3), ('o', 1, 3), ('n', 2, 0), ('n', 2, 1), ('o', 2, 0), ('o', 2, 1), ('n', 2, 2), ('n', 2, 3), ('o', 2, 2), ('o', 2, 3), ('o', 3, 0), ('n', 3, 0), ('n', 3, 1), ('o', 3, 1), ('n', 3, 2), ('n', 3, 3), ('o', 3, 2), ('o', 3, 3)]
-ACC = 5
-BACK = 3
-LEAD = 2
+LOADS = (('w', 0, 0), ('x', 0, 1), ('w', 0, 1), ('x', 1, 2), ('t', 0), ('t', 1), ('t', 2), ('x', 2, 4), ('u', 1), ('x', 4, 6), ('u', 0), ('x', 6, 8), ('w', 1, 0), ('w', 1, 1), ('w', 2, 0), ('w', 2, 1), ('w', 3, 0), ('w', 3, 1))
+SEQ = [('o', 0, 0), ('o', 0, 1), ('o', 0, 2), ('o', 0, 3), ('n', 0, 0), ('n', 0, 1), ('n', 0, 2), ('n', 0, 3), ('o', 1, 0), ('o', 1, 1), ('n', 1, 0), ('n', 1, 1), ('o', 1, 2), ('o', 1, 3), ('n', 1, 2), ('n', 1, 3), ('o', 2, 0), ('n', 2, 0), ('o', 2, 1), ('n', 2, 1), ('o', 2, 2), ('n', 2, 2), ('o', 2, 3), ('n', 2, 3), ('n', 3, 0), ('n', 3, 1), ('o', 3, 0), ('o', 3, 1), ('n', 3, 2), ('n', 3, 3), ('o', 3, 2), ('o', 3, 3)]
+ACC = 4
+BACK = 4
+LEAD = 3
 BLAG = 1
 CLAG = 2
-BATCH = 2
-QUNITS = (((0, 2), (2, 4)), ((0, 2), (2, 4)), ((0, 2), (2, 4)), ((0, 1), (1, 2), (2, 3), (3, 4)))
-VADD = ((3, 2), (3, 3))
-F_SET = (8, 10, 12, 18, 19, 22)
-KBUFS = 4
+BATCH = 1
+QUNITS = (((0, 2), (2, 4)), ((0, 2), (2, 4)), ((0, 2), (2, 4)), ((0, 2), (2, 3), (3, 4)))
+VADD = ((3, 3),)
+F_SET = (8, 9, 12, 18, 20)
+KBUFS = 3
 QBUFS = 5
-HEAD = (('rg', 0, 0, 0, 384, 'V'), ('rg', 0, 0, 384, 512, 'S'), ('tx', 0), ('qp', 0, 0), ('rg', 0, 1, 0, 384, 'V'), ('rg', 0, 1, 384, 512, 'S'), ('ql', 0, 1), ('tx', 1), ('mf', 0, 'S'), ('qp', 0, 1), ('pj', 0), ('tx', 2), ('tx', 3), ('ql', 1, 2), ('pj', 1), ('mf', 1, 'G'), ('ss', 'G'), ('tx', 4), ('tx', 5))
+HEAD = (('rg', 0, 0, 0, 448, 'V'), ('rg', 0, 0, 448, 512, 'S'), ('tx', 0), ('qp', 0, 0), ('rg', 0, 1, 0, 448, 'V'), ('rg', 0, 1, 448, 512, 'S'), ('ql', 0, 1), ('tx', 1), ('mf', 0, 'SS'), ('qp', 0, 1), ('pj', 0), ('tx', 2), ('tx', 3), ('ql', 1, 2), ('pj', 1), ('tx', 4), ('tx', 5))
 PROJECTED = 2
-BEFORE = {1: (('nf', 0), ('nf', 1), ('rg', 1, 0, 256, 512, 'S')), 2: (('rg', 1, 0, 0, 256, 'G'), ('rg', 1, 1, 0, 256, 'S')), 3: (('rg', 1, 1, 256, 512, 'S'), ('rg', 2, 0, 0, 256, 'S')), 4: (('rg', 2, 0, 256, 512, 'S'),), 5: (('rg', 2, 1, 0, 256, 'S'),), 6: (('rg', 2, 1, 256, 512, 'S'),), 12: (('rg', 3, 0, 0, 256, 'S'), ('sf',)), 13: (('rg', 3, 0, 256, 512, 'S'),), 14: (('rg', 3, 1, 0, 256, 'S'),), 15: (('rg', 3, 1, 256, 512, 'S'),)}
-AFTER = {0: (('ql', 2, 4), ('tx', 6), ('tx', 7)), 2: (('qh', 0, 2),), 7: (('qw', 1),), 8: (('qw', 2),), 18: (('qw', 3),)}
-SYNC = {(0, 0): 'hi_grouped', (1, 2): 'w_grouped2'}
-GDELAY = {(0, 1): 2}
-NQ = 0
-LIMIT = {0: 4, 1: 4, 2: 8, 3: 8, 4: 8, 5: 8, 6: 8, 7: 16, 8: 24, 9: 24, 10: 24, 11: 24, 12: 24, 13: 24, 14: 24, 15: 24, 16: 24, 17: 24, 18: 32, 19: 32, 20: 32, 21: 32, 22: 32, 23: 32, 24: 32, 25: 32, 26: 32, 27: 32, 28: 32, 29: 32, 30: 32, 31: 32}
+BEFORE = {0: (('ss', 'G'), ('rg', 1, 0, 0, 256, 'G'), ('rg', 1, 0, 256, 512, 'G')), 2: (('nf', 0), ('nf', 1), ('rg', 1, 1, 256, 512, 'S')), 1: (('rg', 1, 1, 0, 256, 'S'),), 3: (('rg', 2, 0, 0, 256, 'S'),), 4: (('rg', 2, 0, 256, 512, 'S'),), 5: (('rg', 2, 1, 0, 256, 'S'),), 6: (('rg', 2, 1, 256, 512, 'S'),), 12: (('rg', 3, 0, 0, 256, 'S'),), 13: (('rg', 3, 0, 256, 512, 'S'),), 14: (('rg', 3, 1, 0, 256, 'S'),), 15: (('rg', 3, 1, 256, 512, 'S'),), 10: (('sf',),)}
+AFTER = {0: (('ql', 2, 4), ('tx', 6), ('tx', 7)), 2: (('qh', 0, 2),), 3: (('qw', 1),), 12: (('qw', 2),), 19: (('qw', 3),)}
+SYNC = {(0, 0): 'w_grouped1', (1, 2): 'w_grouped2'}
+GDELAY = {(0, 1): 3}
+NQ = 1
+LIMIT = {0: 4, 1: 4, 2: 8, 3: 16, 4: 16, 5: 16, 6: 16, 7: 16, 8: 16, 9: 16, 10: 16, 11: 16, 12: 24, 13: 24, 14: 24, 15: 24, 16: 24, 17: 24, 18: 24, 19: 32, 20: 32, 21: 32, 22: 32, 23: 32, 24: 32, 25: 32, 26: 32, 27: 32, 28: 32, 29: 32, 30: 32, 31: 32}
 
 FLOPS = 2 * 2 * POSITIONS * K * HEADS * CHANNELS
 
@@ -74,7 +74,7 @@ def tile_multiscaleretention_pa_kernel(tc, x, sin, cos, Wq, Wk, out_0, out_1):
         ctx.enter_context(tc.manual_schedule())
 
         x_sb = keep.tile([P, ROW_TILES, K], BF16)
-        tables = [keep.tile([P, 3 * UNIT_TILES * CHANNELS + 2], BF16, name="tables%d" % n) for n in range(HALF_TILES // UNIT_TILES)]
+        tables = keep.tile([P, 3 * HALF_COLS + 2], BF16)
         upper = [keep.tile([P, HALF_TILES, CHANNELS], BF16, name="upper%d" % s) for s in range(2)]
         w_raw = [keep.tile([P, PASSES, PACK, GROUP_COLS], BF16, name="w_raw%d" % g) for g in range(GROUPS)]
         lo_codes = keep.tile([P, HALF_TILES, PASSES, P], U32, align_bytes=64)
@@ -99,14 +99,11 @@ def tile_multiscaleretention_pa_kernel(tc, x, sin, cos, Wq, Wk, out_0, out_1):
             cols = slice((g % 2) * GROUP_COLS, (g % 2 + 1) * GROUP_COLS)
             nc.sync.dma_start(out=w_raw[g][:, c, :, :], in_=w_rows[g // 2][:, c, :, cols])
 
-        def load_tables(part):
-            first, last = part * UNIT_TILES, (part + 1) * UNIT_TILES
-            length = UNIT_TILES * CHANNELS
-            for spot, rows in enumerate((cos_rows, sin_rows, cos_rows)):
-                nc.sync.dma_start(
-                    out=tables[part][:, spot * length : (spot + 1) * length],
-                    in_=rows[:, first * CHANNELS : last * CHANNELS],
-                )
+        def load_tables(spot):
+            nc.sync.dma_start(
+                out=tables[:, spot * HALF_COLS : (spot + 1) * HALF_COLS],
+                in_=(cos_rows, sin_rows, cos_rows)[spot][:, 0:HALF_COLS],
+            )
 
         def load_upper(s):
             nc.sync.dma_start(
@@ -123,19 +120,24 @@ def tile_multiscaleretention_pa_kernel(tc, x, sin, cos, Wq, Wk, out_0, out_1):
         nc.vector.tensor_copy(out=identity_bf[:], in_=identity[:])
 
         def make_factors(part, engine):
-            first, last = part * UNIT_TILES, (part + 1) * UNIT_TILES
-            length = UNIT_TILES * CHANNELS
-            sin_even = tables[part][:, length : 2 * length].rearrange("p (w z) -> p w z", z=2)[:, :, 0]
-            if engine == "G":
-                nc.gpsimd.tensor_scalar(out=sin_even, in0=sin_even, scalar1=-1.0, scalar2=0.0, op0=MULT, op1=ADD)
+            tiles = UNIT_TILES if engine[1:] == "" else HALF_TILES
+            engine = engine[0]
+            first, last = part * UNIT_TILES, part * UNIT_TILES + tiles
+            length = HALF_COLS
+            rows = slice(first * CHANNELS, last * CHANNELS)
+            sin_even = tables[:, length : 2 * length][:, rows].rearrange("p (w z) -> p w z", z=2)[:, :, 0]
+            if engine in "GV":
+                (nc.gpsimd if engine == "G" else nc.vector).tensor_scalar(out=sin_even, in0=sin_even, scalar1=-1.0, scalar2=0.0, op0=MULT, op1=ADD)
             else:
                 nc.scalar.activation(out=sin_even, in_=sin_even, func=COPY, scale=-1.0)
             for source in range(2):
-                both = tables[part][:, source * length : source * length + 2 * (length + 1)].rearrange("p (e w) -> p e w", e=2)
+                both = tables[:, source * length : source * length + 2 * (length + 1)].rearrange("p (e w) -> p e w", e=2)
                 o = factors[:, 0, first:last, source, :].rearrange("p j (i e) -> p j i e", e=2)
-                i = both[:, :, 0:length].rearrange("p e (j i z) -> p j i z e", i=PAIRS, z=2)[:, :, :, 0, :]
+                i = both[:, :, rows].rearrange("p e (j i z) -> p j i z e", i=PAIRS, z=2)[:, :, :, 0, :]
                 if engine == "G":
                     nc.gpsimd.tensor_scalar(out=o, in0=i, scalar1=1.0, scalar2=0.0, op0=MULT, op1=ADD)
+                elif engine == "V":
+                    nc.vector.tensor_copy(out=o, in_=i)
                 else:
                     nc.scalar.copy(out=o, in_=i)
 

from contextlib import ExitStack

import concourse.mybir as mybir
from concourse.masks import make_identity

F32 = mybir.dt.float32
BF16 = mybir.dt.bfloat16
U32 = mybir.dt.uint32
U8 = mybir.dt.uint8
FP8X4 = mybir.dt.float8_e4m3fn_x4
MULT = mybir.AluOpType.mult
ADD = mybir.AluOpType.add
COPY = mybir.ActivationFunctionType.Copy

P = 128
POSITIONS = 1024
K = 1024
HEADS = 8
CHANNELS = 128
PAIRS = CHANNELS // 2
PACK = 4
K_PASS = P * PACK
PASSES = K // K_PASS
ROW_TILES = POSITIONS // P
HALF_TILES = ROW_TILES // 2
HALVES = 2
HALF_COLS = HALF_TILES * P
GROUP_HEADS = 4
GROUP_COLS = GROUP_HEADS * CHANNELS
RUN = 4
GROUPS = 2 * HEADS // GROUP_HEADS
UNIT_TILES = 2
K_SCALE = CHANNELS**-0.5
VECTOR_COLS = 320
LOADS = (('w', 0, 0), ('x', 0, 1), ('w', 0, 1), ('x', 1, 2), ('t', 0), ('t', 1), ('t', 2), ('x', 2, 4), ('u', 1), ('x', 4, 6), ('u', 0), ('x', 6, 8), ('w', 1, 0), ('w', 1, 1), ('w', 2, 0), ('w', 2, 1), ('w', 3, 0), ('w', 3, 1))
SEQ = [('o', 0, 0), ('o', 0, 1), ('o', 0, 2), ('o', 0, 3), ('n', 0, 0), ('n', 0, 1), ('n', 0, 2), ('n', 0, 3), ('o', 1, 0), ('o', 1, 1), ('n', 1, 0), ('n', 1, 1), ('o', 1, 2), ('o', 1, 3), ('n', 1, 2), ('n', 1, 3), ('o', 2, 0), ('n', 2, 0), ('o', 2, 1), ('n', 2, 1), ('o', 2, 2), ('n', 2, 2), ('o', 2, 3), ('n', 2, 3), ('n', 3, 0), ('n', 3, 1), ('o', 3, 0), ('o', 3, 1), ('n', 3, 2), ('n', 3, 3), ('o', 3, 2), ('o', 3, 3)]
ACC = 4
BACK = 4
LEAD = 3
BLAG = 1
CLAG = 2
BATCH = 1
QUNITS = (((0, 2), (2, 4)), ((0, 2), (2, 4)), ((0, 2), (2, 4)), ((0, 2), (2, 3), (3, 4)))
VADD = ((3, 3),)
F_SET = (8, 9, 12, 18, 20)
KBUFS = 3
QBUFS = 5
HEAD = (('rg', 0, 0, 0, 448, 'V'), ('rg', 0, 0, 448, 512, 'S'), ('tx', 0), ('qp', 0, 0), ('rg', 0, 1, 0, 448, 'V'), ('rg', 0, 1, 448, 512, 'S'), ('ql', 0, 1), ('tx', 1), ('mf', 0, 'SS'), ('qp', 0, 1), ('pj', 0), ('tx', 2), ('tx', 3), ('ql', 1, 2), ('pj', 1), ('tx', 4), ('tx', 5))
PROJECTED = 2
BEFORE = {0: (('ss', 'G'), ('rg', 1, 0, 0, 256, 'G'), ('rg', 1, 0, 256, 512, 'G')), 2: (('nf', 0), ('nf', 1), ('rg', 1, 1, 256, 512, 'S')), 1: (('rg', 1, 1, 0, 256, 'S'),), 3: (('rg', 2, 0, 0, 256, 'S'),), 4: (('rg', 2, 0, 256, 512, 'S'),), 5: (('rg', 2, 1, 0, 256, 'S'),), 6: (('rg', 2, 1, 256, 512, 'S'),), 12: (('rg', 3, 0, 0, 256, 'S'),), 13: (('rg', 3, 0, 256, 512, 'S'),), 14: (('rg', 3, 1, 0, 256, 'S'),), 15: (('rg', 3, 1, 256, 512, 'S'),), 10: (('sf',),)}
AFTER = {0: (('ql', 2, 4), ('tx', 6), ('tx', 7)), 2: (('qh', 0, 2),), 3: (('qw', 1),), 12: (('qw', 2),), 19: (('qw', 3),)}
SYNC = {(0, 0): 'w_grouped1', (1, 2): 'w_grouped2'}
GDELAY = {(0, 1): 3}
NQ = 1
LIMIT = {0: 4, 1: 4, 2: 8, 3: 16, 4: 16, 5: 16, 6: 16, 7: 16, 8: 16, 9: 16, 10: 16, 11: 16, 12: 24, 13: 24, 14: 24, 15: 24, 16: 24, 17: 24, 18: 24, 19: 32, 20: 32, 21: 32, 22: 32, 23: 32, 24: 32, 25: 32, 26: 32, 27: 32, 28: 32, 29: 32, 30: 32, 31: 32}

FLOPS = 2 * 2 * POSITIONS * K * HEADS * CHANNELS


def tile_multiscaleretention_pa_kernel(tc, x, sin, cos, Wq, Wk, out_0, out_1):
    nc = tc.nc
    x_rows = x.flatten_outer_dims().rearrange("(p j) k -> p j k", j=ROW_TILES)
    cos_rows = cos.rearrange("(p j) d -> p (j d)", j=ROW_TILES)
    sin_rows = sin.rearrange("(p j) d -> p (j d)", j=ROW_TILES)
    o_rows = [o.rearrange("b h (p j) d -> p (b h) j d", j=ROW_TILES) for o in (out_0, out_1)]
    n_rows = [o.rearrange("b h (p f j) d -> p (b h) f (j d)", f=HALVES, j=HALF_TILES) for o in (out_0, out_1)]
    w_rows = [w.rearrange("(c p t) n -> p c t n", c=PASSES, t=PACK) for w in (Wq, Wk)]

    with ExitStack() as ctx:
        keep = ctx.enter_context(tc.tile_pool(name="keep", bufs=1))
        stage = ctx.enter_context(tc.tile_pool(name="stage", bufs=3))
        psum_acc = ctx.enter_context(tc.psum_pool(name="psum_acc", bufs=ACC))
        psum_back = ctx.enter_context(tc.psum_pool(name="psum_back", bufs=BACK))
        ctx.enter_context(tc.manual_schedule())

        x_sb = keep.tile([P, ROW_TILES, K], BF16)
        tables = keep.tile([P, 3 * HALF_COLS + 2], BF16)
        upper = [keep.tile([P, HALF_TILES, CHANNELS], BF16, name="upper%d" % s) for s in range(2)]
        w_raw = [keep.tile([P, PASSES, PACK, GROUP_COLS], BF16, name="w_raw%d" % g) for g in range(GROUPS)]
        lo_codes = keep.tile([P, HALF_TILES, PASSES, P], U32, align_bytes=64)
        lo_scales = keep.tile([P, HALF_TILES, PASSES, P], U8, align_bytes=64)
        hi_codes = keep.tile([P, PASSES, HALF_COLS], U32, align_bytes=64)
        hi_scales = keep.tile([P, PASSES, HALF_COLS], U8, align_bytes=64)
        w_codes = keep.tile([P, GROUPS, PASSES, GROUP_COLS], U32, align_bytes=64)
        w_scales = keep.tile([P, GROUPS, PASSES, GROUP_COLS], U8, align_bytes=64)
        factors = keep.tile([P, 2, HALF_TILES, 2, CHANNELS], F32)
        n_factors = keep.tile([P, 2, HALF_COLS], F32)
        partner_sin = keep.tile([P, HALF_TILES, CHANNELS], BF16)
        identity = keep.tile([P, P], F32)
        swap = keep.tile([P, P], F32)
        identity_bf = keep.tile([P, P], BF16)
        w_grouped = {}
        half = GROUP_COLS // 2

        def load_x(first, last):
            nc.sync.dma_start(out=x_sb[:, first:last, :], in_=x_rows[:, first:last, :])

        def load_w(g, c):
            cols = slice((g % 2) * GROUP_COLS, (g % 2 + 1) * GROUP_COLS)
            nc.sync.dma_start(out=w_raw[g][:, c, :, :], in_=w_rows[g // 2][:, c, :, cols])

        def load_tables(spot):
            nc.sync.dma_start(
                out=tables[:, spot * HALF_COLS : (spot + 1) * HALF_COLS],
                in_=(cos_rows, sin_rows, cos_rows)[spot][:, 0:HALF_COLS],
            )

        def load_upper(s):
            nc.sync.dma_start(
                out=upper[s][:].rearrange("p j d -> p (j d)"),
                in_=(cos_rows, sin_rows)[s][:, HALF_TILES * CHANNELS : ROW_TILES * CHANNELS],
            )

        for what in LOADS:
            {"x": load_x, "w": load_w, "t": load_tables, "u": load_upper}[what[0]](*what[1:])

        make_identity(nc, identity[:])
        nc.vector.tensor_copy(out=swap[:, 0:P:2], in_=identity[:, 1:P:2])
        nc.vector.tensor_copy(out=swap[:, 1:P:2], in_=identity[:, 0:P:2])
        nc.vector.tensor_copy(out=identity_bf[:], in_=identity[:])

        def make_factors(part, engine):
            tiles = UNIT_TILES if engine[1:] == "" else HALF_TILES
            engine = engine[0]
            first, last = part * UNIT_TILES, part * UNIT_TILES + tiles
            length = HALF_COLS
            rows = slice(first * CHANNELS, last * CHANNELS)
            sin_even = tables[:, length : 2 * length][:, rows].rearrange("p (w z) -> p w z", z=2)[:, :, 0]
            if engine in "GV":
                (nc.gpsimd if engine == "G" else nc.vector).tensor_scalar(out=sin_even, in0=sin_even, scalar1=-1.0, scalar2=0.0, op0=MULT, op1=ADD)
            else:
                nc.scalar.activation(out=sin_even, in_=sin_even, func=COPY, scale=-1.0)
            for source in range(2):
                both = tables[:, source * length : source * length + 2 * (length + 1)].rearrange("p (e w) -> p e w", e=2)
                o = factors[:, 0, first:last, source, :].rearrange("p j (i e) -> p j i e", e=2)
                i = both[:, :, rows].rearrange("p e (j i z) -> p j i z e", i=PAIRS, z=2)[:, :, :, 0, :]
                if engine == "G":
                    nc.gpsimd.tensor_scalar(out=o, in0=i, scalar1=1.0, scalar2=0.0, op0=MULT, op1=ADD)
                elif engine == "V":
                    nc.vector.tensor_copy(out=o, in_=i)
                else:
                    nc.scalar.copy(out=o, in_=i)

        def scale_factors():
            nc.scalar.activation(
                out=factors[:, 1].rearrange("p j s d -> p (j s d)"),
                in_=factors[:, 0].rearrange("p j s d -> p (j s d)"),
                func=COPY,
                scale=K_SCALE,
            )

        def swap_sin(engine):
            for e in range(2):
                o, i, f = partner_sin[:, :, e::2], upper[1][:, :, 1 - e :: 2], 1.0 - 2.0 * e
                if engine == "G":
                    nc.gpsimd.tensor_scalar(out=o, in0=i, scalar1=f, scalar2=0.0, op0=MULT, op1=ADD)
                elif engine == "V":
                    nc.vector.tensor_scalar(out=o, in0=i, scalar1=f, scalar2=0.0, op0=MULT, op1=ADD)
                else:
                    nc.scalar.activation(out=o, in_=i, func=COPY, scale=f)

        def make_n_factors(s):
            turned = psum_back.tile([P, HALF_TILES, P], BF16, name="back")
            for jj in range(HALF_TILES):
                nc.tensor.transpose(turned[:, jj, :], (partner_sin if s else upper[0])[:, jj, :], identity_bf[:])
            nc.scalar.copy(out=n_factors[:, s, :], in_=turned[:].rearrange("p j r -> p (j r)"))

        x_grouped = {}

        def transpose_x(j):
            words = x_sb[:, j, :].bitcast(F32)
            turned = psum_back.tile([P, PASSES, 2, P], F32, name="back")
            for c in range(PASSES):
                for u in range(2):
                    first = c * (K_PASS // 2) + u
                    nc.tensor.transpose(turned[:, c, u, :], words[:, first : (c + 1) * (K_PASS // 2) : 2], identity[:])
            if j < HALF_TILES:
                pair, jj = divmod(j, UNIT_TILES)
                if jj == 0:
                    x_grouped[pair] = stage.tile([P, UNIT_TILES, K], BF16, align_bytes=64, name="lo_grouped%d" % pair, bufs=1)
                out = x_grouped[pair][:, jj].bitcast(F32).rearrange("p (c r u) -> p c r u", c=PASSES, u=2)
            else:
                if j == HALF_TILES:
                    x_grouped[2] = stage.tile([P, PASSES, HALF_TILES, P * PACK], BF16, align_bytes=64, name="hi_grouped", bufs=1)
                out = x_grouped[2][:, :, j - HALF_TILES, :].bitcast(F32).rearrange("p c (r u) -> p c r u", u=2)
            nc.scalar.copy(out=out, in_=turned[:].rearrange("p c u r -> p c r u"))

        def quantise_lo(first, last):
            pair = first // UNIT_TILES
            nc.vector.quantize_mx(
                out=lo_codes[:, first:last].rearrange("p j c r -> p (j c r)").bitcast(FP8X4),
                scales=lo_scales[:, first:last].rearrange("p j c r -> p (j c r)"),
                in_=x_grouped[pair][:, first - pair * UNIT_TILES : last - pair * UNIT_TILES].rearrange("p j k -> p (j k)"),
            )

        def quantise_hi(first, last):
            nc.vector.quantize_mx(
                out=hi_codes[:, first:last].rearrange("p c r -> p (c r)").bitcast(FP8X4),
                scales=hi_scales[:, first:last].rearrange("p c r -> p (c r)"),
                in_=x_grouped[2][:, first:last].rearrange("p c j k -> p (c j k)"),
            )

        def regroup_w(g, c, first, last, engine):
            if g not in w_grouped:
                w_grouped[g] = stage.tile([P, PASSES, GROUP_COLS, PACK], BF16, align_bytes=64, name="w_grouped%d" % g, bufs=1)
            cols = slice(first, last)
            out, src = w_grouped[g][:, c, cols, :], w_raw[g][:, c, :, cols]
            if engine == "G":
                nc.gpsimd.tensor_scalar(
                    out=out, in0=src.rearrange("p t n -> p n t"), scalar1=1.0, scalar2=0.0, op0=MULT, op1=ADD
                )
            else:
                (nc.vector.tensor_copy if engine == "V" else nc.scalar.copy)(
                    out=out.rearrange("p (n r) t -> p n t r", r=RUN), in_=src.rearrange("p t (n r) -> p n t r", r=RUN)
                )

        def quantise_w(g):
            nc.vector.quantize_mx(
                out=w_codes[:, g].rearrange("p c n -> p (c n)").bitcast(FP8X4),
                scales=w_scales[:, g].rearrange("p c n -> p (c n)"),
                in_=w_grouped[g][:].rearrange("p c n t -> p (c n t)"),
            )

        def quantise_w_pass(g, c):
            nc.vector.quantize_mx(
                out=w_codes[:, g, c, :].bitcast(FP8X4),
                scales=w_scales[:, g, c, :],
                in_=w_grouped[g][:, c].rearrange("p n t -> p (n t)"),
            )

        sums = {}

        def project(n):
            item = SEQ[n]
            acc = psum_acc.tile([P, GROUP_COLS], F32, name="acc")
            for c in range(PASSES):
                if item[0] == "o":
                    g, j = item[1:]
                    ops = (lo_codes[:, j, c, :], lo_scales[:, j, c, :], w_codes[:, g, c, :], w_scales[:, g, c, :])
                else:
                    g, h = item[1:]
                    rows = slice(h * CHANNELS, (h + 1) * CHANNELS)
                    ops = (w_codes[:, g, c, rows], w_scales[:, g, c, rows], hi_codes[:, c, :], hi_scales[:, c, :])
                nc.tensor.matmul_mx(
                    out=acc[:],
                    lhsT=ops[0].bitcast(FP8X4),
                    lhsT_scale=ops[1],
                    rhs=ops[2].bitcast(FP8X4),
                    rhs_scale=ops[3],
                    start=(c == 0),
                    stop=(c == PASSES - 1),
                )
            sums[n] = acc

        shares = {}
        q_units = {}

        def unit_of(j, g):
            for a, b in QUNITS[g]:
                if a <= j < b:
                    return a, b

        def multiply(n):
            item = SEQ[n]
            if item[0] == "n":
                shares[n] = stage.tile([P, 2, HALF_COLS], F32, name="shares", bufs=KBUFS)
                if n in F_SET:
                    nc.vector.tensor_tensor(out=shares[n][:, 0, :], in0=sums[n][:], in1=n_factors[:, 0, :], op=MULT)
                    lifted = stage.tile([P, HALF_COLS], F32, name="lifted", bufs=2)
                    nc.scalar.copy(out=lifted[:], in_=sums[n][:])
                    nc.gpsimd.tensor_tensor(out=shares[n][:, 1, :], in0=lifted[:], in1=n_factors[:, 1, :], op=MULT)
                    return
                nc.vector.tensor_tensor(
                    out=shares[n][:],
                    in0=sums[n][:].unsqueeze(1).to_broadcast([P, 2, HALF_COLS]),
                    in1=n_factors[:],
                    op=MULT,
                )
                return
            g, j = item[1:]
            a, b = unit_of(j, g)
            if j == a:
                q_units[g, a] = stage.tile([P, 2, GROUP_HEADS, b - a, CHANNELS], F32, name="q_units", bufs=QBUFS)
            unit = q_units[g, a]
            if n in F_SET:
                shape = [P, GROUP_HEADS, PAIRS, 2]
                nc.vector.tensor_tensor(
                    out=unit[:, 0, :, j - a, :].rearrange("p h (i e) -> p h i e", e=2),
                    in0=sums[n][:].rearrange("p (h i s) -> p s h i", h=GROUP_HEADS, s=2)[:, 0].unsqueeze(3).to_broadcast(shape),
                    in1=factors[:, g // 2, j, 0].rearrange("p (i e) -> p i e", e=2).unsqueeze(1).to_broadcast(shape),
                    op=MULT,
                )
                odd = stage.tile([P, GROUP_COLS // 2], F32, name="odd", bufs=3)
                nc.scalar.copy(out=odd[:], in_=sums[n][:, 1::2])
                nc.gpsimd.tensor_tensor(
                    out=unit[:, 1, :, j - a, :].rearrange("p h (i e) -> p h i e", e=2),
                    in0=odd[:].rearrange("p (h i) -> p h i", h=GROUP_HEADS).unsqueeze(3).to_broadcast(shape),
                    in1=factors[:, g // 2, j, 1].rearrange("p (i e) -> p i e", e=2).unsqueeze(1).to_broadcast(shape),
                    op=MULT,
                )
                return
            shape = [P, 2, GROUP_HEADS, PAIRS, 2]
            nc.vector.tensor_tensor(
                out=unit[:, :, :, j - a, :].rearrange("p s h (i e) -> p s h i e", e=2),
                in0=sums[n][:].rearrange("p (h i s) -> p s h i", h=GROUP_HEADS, s=2).unsqueeze(4).to_broadcast(shape),
                in1=factors[:, g // 2, j].rearrange("p s (i e) -> p s i e", e=2).unsqueeze(2).to_broadcast(shape),
                op=MULT,
            )

        def add_q(n):
            g, j = SEQ[n][1:]
            a, b = unit_of(j, g)
            unit = q_units[g, a]
            result = unit[:, 0]
            if (g, a) in SYNC:
                result = stage.tile([P, GROUP_HEADS, b - a, CHANNELS], F32, align_bytes=64, name=SYNC[g, a], bufs=1)
            engine = nc.vector if (g, a) in VADD else nc.gpsimd
            engine.tensor_tensor(out=result[:], in0=unit[:, 0], in1=unit[:, 1], op=ADD)
            nc.sync.dma_start(out=o_rows[g // 2][:, g % 2 * GROUP_HEADS : (g % 2 + 1) * GROUP_HEADS, a:b, :], in_=result[:])

        backs = {}

        def turn_back(n):
            back = psum_back.tile([P, HALF_TILES, CHANNELS], F32, name="back")
            for jj in range(HALF_TILES):
                cols = slice(jj * P, (jj + 1) * P)
                nc.tensor.matmul(out=back[:, jj, :], lhsT=shares[n][:, 0, cols], rhs=identity[:], is_transpose=True, start=True, stop=False)
                nc.tensor.matmul(out=back[:, jj, :], lhsT=shares[n][:, 1, cols], rhs=swap[:], is_transpose=True, start=False, stop=True)
            backs[n] = back

        def copy_back(n):
            g, h = SEQ[n][1:]
            result = stage.tile([P, HALF_TILES * CHANNELS], F32, name="result", bufs=4)
            flat = backs[n][:].rearrange("p j d -> p (j d)")
            if g < 2:
                nc.scalar.copy(out=result[:], in_=flat)
            else:
                nc.scalar.activation(out=result[:], in_=flat, func=COPY, scale=K_SCALE)
            (nc.scalar if NQ else nc.sync).dma_start(out=n_rows[g // 2][:, g % 2 * GROUP_HEADS + h, 1, :], in_=result[:])

        ops = {
            "rg": regroup_w, "tx": transpose_x, "ql": quantise_lo, "qh": quantise_hi, "qw": quantise_w, "qp": quantise_w_pass, "mf": make_factors,
            "sf": scale_factors, "ss": swap_sin, "nf": make_n_factors, "pj": project,
        }

        def run(todo):
            for op in todo:
                ops[op[0]](*op[1:])

        done, late = [], []
        run(HEAD)
        projected = PROJECTED
        for n in range(len(SEQ)):
            run(BEFORE.get(n, ()))
            multiply(n)
            run(AFTER.get(n, ()))
            while projected < min(len(SEQ), n + LEAD + 1) and projected < LIMIT.get(n, 99):
                project(projected)
                projected += 1
            waiting = [m for m in range(n + 1) if SEQ[m][0] == "n" and m not in backs and m <= n - BLAG]
            if len(waiting) >= BATCH or n == len(SEQ) - 1 or (waiting and max(m for m in range(len(SEQ)) if SEQ[m][0] == "n") <= n):
                for m in [m for m in range(n + 1) if SEQ[m][0] == "n" and m not in backs] if n == len(SEQ) - 1 else waiting:
                    turn_back(m)
            for m in sorted(backs):
                if m not in done and (m <= n - CLAG or n == len(SEQ) - 1):
                    copy_back(m)
                    done.append(m)
            if SEQ[n][0] == "o":
                g, j = SEQ[n][1:]
                if j + 1 == unit_of(j, g)[1]:
                    late.append(n)
            for m in late[:]:
                if GDELAY.get(SEQ[m][1:], m) <= n:
                    add_q(m)
                    late.remove(m)
